import numpy as np
import ml_dtypes


def mxq(x, axis, fmt="e4m3"):
    dtype, down = {"e4m3": (ml_dtypes.float8_e4m3fn, 7), "e5m2": (ml_dtypes.float8_e5m2, 14)}[fmt]
    v = np.moveaxis(np.asarray(x, np.float32).astype(ml_dtypes.bfloat16).astype(np.float64), axis, -1)
    blocks = v.reshape(v.shape[:-1] + (-1, 32))
    amax = np.abs(blocks).max(-1, keepdims=True)
    byte = np.maximum(np.where(amax > 0, np.frexp(amax)[1] - 1 + 127, 0) - down, 1)
    scale = np.exp2(byte - 127.0)
    codes = (blocks / scale).astype(np.float32).astype(dtype).astype(np.float64)
    return np.moveaxis((codes * scale).reshape(v.shape), -1, axis)


WIDE = False


def mx_kscale(k):
    if not WIDE:
        return np.ones(k)
    levels = np.array([10, -10, 5, -5, 0])
    a = np.random.permutation(np.resize(levels, k // 512 * 4)).reshape(k // 512, 4)
    idx = np.arange(k)
    return np.exp2(a[idx // 512, idx % 128 // 32])


BF16 = ml_dtypes.bfloat16


def bf(x):
    return np.asarray(x, np.float32).astype(BF16)


def f64(x):
    return np.asarray(x).astype(np.float64)


E2M1 = np.array([0.0, 0.5, 1.0, 1.5, 2.0, 3.0, 4.0, 6.0, -0.0, -0.5, -1.0, -1.5, -2.0, -3.0, -4.0, -6.0])


def pack_weight(w, fmt):
    k, n = w.shape
    w = f64(bf(w)).reshape(k // 32, 32, n)
    amax = np.abs(w).max(1)
    if fmt == "e4m3":
        byte = np.frexp(amax)[1] - 1 + 127 - 7
    else:
        mant, ex = np.frexp(amax / 6.0)
        byte = np.where(mant > 0.5, ex, ex - 1) + 127
    byte = np.clip(np.where(amax > 0, byte, 1), 1, 254)
    scaled = (w * np.exp2(127.0 - byte)[:, None, :]).reshape(k, n).astype(np.float32)
    by_word = np.ascontiguousarray(scaled.reshape(k // 512, 128, 4, n).transpose(0, 1, 3, 2))
    if fmt == "e4m3":
        words = by_word.astype(ml_dtypes.float8_e4m3fn).view(np.uint8)
    else:
        c = by_word.astype(ml_dtypes.float4_e2m1fn).view(np.uint8) & 0xF
        words = c[..., 0::2] | (c[..., 1::2] << 4)
    return np.ascontiguousarray(words), np.ascontiguousarray(byte.astype(np.uint8).reshape(k // 512, 16, n))


def unpack_weight(words, scales, fmt):
    g, p, n, _ = words.shape
    if fmt == "e4m3":
        vals = np.ascontiguousarray(words).view(ml_dtypes.float8_e4m3fn).astype(np.float64)
    else:
        nib = np.empty((g, p, n, 4), np.uint8)
        nib[..., 0::2] = words & 0xF
        nib[..., 1::2] = words >> 4
        vals = E2M1[nib]
    vals = vals * np.repeat(np.exp2(scales.astype(np.float64) - 127.0), 8, axis=1)[..., None]
    return vals.transpose(0, 1, 3, 2).reshape(g * 512, n)


B, LQ, LK, DIN, H = 2, 512, 512, 8192, 256
FLOOR = 1e-9
FMT = "e4m3"


def setup_inputs():
    s = mx_kscale(DIN)
    mass = np.where(np.random.random((B, LQ, 1)) < 0.25, FLOOR, 1.0)
    q = bf(np.random.standard_normal((B, LQ, H)) * 1.5)
    k = bf(np.random.standard_normal((B, LK, H)) * 1.5)
    v_ret = bf(np.random.standard_normal((B, LK, DIN)) * s)
    pi_star = bf(mass * np.exp(1.25 * np.random.standard_normal((B, LQ, LK))))
    Wv_words, Wv_scales = pack_weight(np.random.standard_normal((DIN, H)) * 1.5 / np.sqrt(DIN) / s[:, None], FMT)
    bv = bf(np.random.standard_normal(H) * 0.25)
    gamma = bf(1.25 + 0.25 * np.random.random(1))
    return {"q": q,
            "k": k,
            "v_ret": v_ret,
            "pi_star": pi_star,
            "Wv_words": Wv_words,
            "Wv_scales": Wv_scales,
            "bv": bv,
            "gamma": gamma}


def reference(q, k, v_ret, pi_star, Wv_words, Wv_scales, bv, gamma):
    wvq = unpack_weight(Wv_words, Wv_scales, FMT)
    rows = []
    for b in range(B):
        v = (mxq(f64(v_ret[b]), 1, "e4m3") @ wvq) + f64(bv)
        logits = f64(q[b]) @ f64(k[b]).T / np.sqrt(H)
        z = logits + f64(gamma) * np.log(np.maximum(f64(pi_star[b]), FLOOR))
        e = np.exp(z - z.max(1, keepdims=True))
        rows.append((mxq(e, 1, "e4m3") @ mxq(v, 0, "e4m3")) / e.sum(1, keepdims=True))
    return np.stack(rows)

@@ -1,0 +1,339 @@
+from contextlib import ExitStack
+
+import concourse.mybir as mybir
+from concourse.masks import make_identity
+
+F32 = mybir.dt.float32
+BF16 = mybir.dt.bfloat16
+I32 = mybir.dt.int32
+U32 = mybir.dt.uint32
+U8 = mybir.dt.uint8
+FP8X4 = mybir.dt.float8_e4m3fn_x4
+ALU = mybir.AluOpType
+ACT = mybir.ActivationFunctionType
+AXIS = mybir.AxisListType
+
+B, LQ, LK, DIN, H = 2, 512, 512, 8192, 256
+FLOOR = 1e-9
+SQRT_H = 16.0
+
+P = 128
+PACK = 4
+K_PASS = P * PACK
+GROUPS = DIN // K_PASS
+BLOCKS = LK // P
+UNITS = B * BLOCKS
+H_HALVES = H // P
+
+ROUND_GROUPS = 8
+ROUNDS_PER_BLOCK = GROUPS // ROUND_GROUPS
+ROUNDS = B * BLOCKS * ROUNDS_PER_BLOCK
+ROUNDS_PER_BATCH = ROUNDS // B
+ROUND_FEATURES = ROUND_GROUPS * K_PASS
+BANK_GROUPS = 2
+ROUND_BANKS = ROUND_GROUPS // BANK_GROUPS
+QUANT_GROUPS = 4
+X_BUFS = 8
+
+FLOPS = 2 * B * LK * DIN * H + 2 * B * LQ * LK * H + 2 * B * LQ * LK * H
+
+
+def tile_pgwcrossattention_pa_k_kernel(
+    tc, q, k, v_ret, pi_star, Wv_words, Wv_scales, bv, gamma, out
+):
+    nc = tc.nc
+    with ExitStack() as ctx:
+        ctx.enter_context(tc.manual_schedule())
+        keep = ctx.enter_context(tc.tile_pool(name="keep", bufs=1))
+        x_pool = ctx.enter_context(tc.tile_pool(name="x", bufs=X_BUFS))
+        stage = ctx.enter_context(tc.tile_pool(name="stage", bufs=3))
+        batch_pool = ctx.enter_context(tc.tile_pool(name="batch", bufs=B))
+        xt_psum = ctx.enter_context(tc.psum_pool(name="xt_psum", bufs=ROUND_BANKS))
+        v_psum = ctx.enter_context(tc.psum_pool(name="v_psum", bufs=2))
+        small_psum = ctx.enter_context(tc.psum_pool(name="small_psum", bufs=2))
+
+        ident_f32 = keep.tile([P, P], F32, name="ident_f32")
+        make_identity(nc, ident_f32[:])
+        ident_bf = keep.tile([P, P], BF16, name="ident_bf")
+        make_identity(nc, ident_bf[:])
+
+        w_scales = keep.tile([P, GROUPS, H], U8, name="w_scales", align_bytes=64)
+        nc.vector.memset(w_scales[:].rearrange("p g n -> p (g n)").bitcast(I32), 0)
+        for first in range(2):
+            for row in range(4):
+                nc.sync.dma_start(
+                    out=w_scales[32 * first + row : P : 64].bitcast(I32),
+                    in_=Wv_scales[:, 4 * first + row : 16 : 8, :]
+                    .rearrange("g c n -> c g n")
+                    .bitcast(I32),
+                )
+
+        pi_sb = keep.tile([P, B, BLOCKS, LK], BF16, name="pi_sb")
+        nc.sync.dma_start(out=pi_sb[:], in_=pi_star.rearrange("b (p j) c -> p b j c", j=BLOCKS))
+        k_sb = keep.tile([P, B, BLOCKS, H], BF16, name="k_sb")
+        nc.sync.dma_start(out=k_sb[:], in_=k.rearrange("b (p t) h -> p b t h", t=BLOCKS))
+        q_sb = keep.tile([P, B, BLOCKS, H], BF16, name="q_sb")
+        nc.sync.dma_start(out=q_sb[:], in_=q.rearrange("b (p j) h -> p b j h", j=BLOCKS))
+
+        gamma_bf = keep.tile([P, 1], BF16, name="gamma_bf")
+        nc.scalar.dma_start(out=gamma_bf[:], in_=gamma.partition_broadcast(P))
+        bv_bf = keep.tile([P, H], BF16, name="bv_bf")
+        nc.scalar.dma_start(out=bv_bf[:], in_=bv.partition_broadcast(P))
+
+        w_words = keep.tile([P, GROUPS, H], U32, name="w_words", align_bytes=64)
+
+        def load_w(part):
+            groups = slice(part * ROUND_GROUPS, (part + 1) * ROUND_GROUPS)
+            nc.sync.dma_start(
+                out=w_words[:, groups, :].bitcast(I32),
+                in_=Wv_words[groups].rearrange("g p n t -> p g (n t)").bitcast(I32),
+            )
+
+        x_tiles = {}
+
+        def load_x(r):
+            block, part = divmod(r, ROUNDS_PER_BLOCK)
+            b, t = divmod(block, BLOCKS)
+            x_sb = x_pool.tile([P, ROUND_FEATURES], BF16, name="x_sb")
+            nc.sync.dma_start(
+                out=x_sb[:],
+                in_=v_ret[b].rearrange("(p t) f -> p t f", t=BLOCKS)[
+                    :, t, part * ROUND_FEATURES : (part + 1) * ROUND_FEATURES
+                ],
+            )
+            x_tiles[r] = x_sb
+
+        load_x(0)
+        load_x(1)
+        load_w(0)
+        load_x(2)
+        load_w(1)
+        for r in range(3, X_BUFS - 1):
+            load_x(r)
+
+        gamma16 = keep.tile([P, 1], F32, name="gamma16")
+        nc.vector.tensor_scalar_mul(out=gamma16[:], in0=gamma_bf[:], scalar1=SQRT_H)
+
+        log_pi = keep.tile([P, UNITS, LK], F32, name="log_pi")
+        for unit in range(UNITS):
+            b, j = divmod(unit, BLOCKS)
+            nc.vector.tensor_scalar_max(
+                out=log_pi[:, unit, :].rearrange("p (t c) -> p t c", t=BLOCKS),
+                in0=pi_sb[:, b, j, :].rearrange("p (c t) -> p t c", t=BLOCKS),
+                scalar1=FLOOR,
+            )
+            nc.scalar.activation(out=log_pi[:, unit, :], in_=log_pi[:, unit, :], func=ACT.Ln)
+
+        def transpose_rows(rows_sb, name):
+            flipped = keep.tile([P, B, H_HALVES, LK], BF16, name=name)
+            for b in range(B):
+                bank = xt_psum.tile([P, H_HALVES, BLOCKS, P], BF16, name="qk_bank", tag="xt")
+                for a in range(H_HALVES):
+                    for i in range(BLOCKS):
+                        nc.tensor.transpose(
+                            bank[:, a, i, :], rows_sb[:, b, i, a * P : (a + 1) * P], ident_bf[:]
+                        )
+                nc.vector.tensor_copy(
+                    out=flipped[:, b], in_=bank[:].rearrange("p a i c -> p a (i c)")
+                )
+            return flipped
+
+        kT = transpose_rows(k_sb, "kT")
+        qT = transpose_rows(q_sb, "qT")
+
+        grouped_tiles = {}
+        x_codes = {}
+        x_scales = {}
+
+        def transpose_round(r):
+            x_words = x_tiles[r][:].bitcast(F32)
+            grouped = stage.tile([P, ROUND_GROUPS * P * PACK], BF16, name="grouped", align_bytes=64)
+            grouped_words = grouped[:].bitcast(F32).rearrange(
+                "p (a g c u) -> p a g c u", a=ROUND_BANKS, g=BANK_GROUPS, u=2
+            )
+            for a in range(ROUND_BANKS):
+                bank = xt_psum.tile([P, BANK_GROUPS, 2, P], F32, name="xt_bank", tag="xt")
+                for g in range(BANK_GROUPS):
+                    first_word = (a * BANK_GROUPS + g) * (K_PASS // 2)
+                    for u in range(2):
+                        nc.tensor.transpose(
+                            bank[:, g, u, :],
+                            x_words[:, first_word + u : first_word + K_PASS // 2 : 2],
+                            ident_f32[:],
+                        )
+                nc.scalar.copy(
+                    out=grouped_words[:, a], in_=bank[:].rearrange("p g u c -> p g c u")
+                )
+            grouped_tiles[r] = grouped
+
+        def quantise_round(r):
+            grouped = grouped_tiles[r]
+            codes = stage.tile([P, ROUND_GROUPS * P], U32, name="codes", align_bytes=64)
+            scales = stage.tile([P, ROUND_GROUPS * P], U8, name="scales", align_bytes=64)
+            width = QUANT_GROUPS * P
+            for i in range(ROUND_GROUPS // QUANT_GROUPS):
+                nc.vector.quantize_mx(
+                    out=codes[:, i * width : (i + 1) * width].bitcast(FP8X4),
+                    scales=scales[:, i * width : (i + 1) * width],
+                    in_=grouped[:, i * width * PACK : (i + 1) * width * PACK],
+                )
+            x_codes[r] = codes
+            x_scales[r] = scales
+
+        v_banks = {}
+        v_grouped = {}
+        v_codes = {}
+        v_scales = {}
+
+        def passes_round(r):
+            block, part = divmod(r, ROUNDS_PER_BLOCK)
+            b, t = divmod(block, BLOCKS)
+            if part == 0 and t % 2 == 0:
+                v_banks[b] = v_psum.tile([P, 2, H], F32, name="v_bank")
+            codes = x_codes[r]
+            scales = x_scales[r]
+            for i in range(ROUND_GROUPS):
+                g = part * ROUND_GROUPS + i
+                nc.tensor.matmul_mx(
+                    out=v_banks[b][:, t % 2, :],
+                    lhsT=codes[:, i * P : (i + 1) * P].bitcast(FP8X4),
+                    lhsT_scale=scales[:, i * P : (i + 1) * P],
+                    rhs=w_words[:, g, :].bitcast(FP8X4),
+                    rhs_scale=w_scales[:, g, :],
+                    start=(g == 0),
+                    stop=(g == GROUPS - 1),
+                )
+            if part == ROUNDS_PER_BLOCK - 1 and t % 2 == 1:
+                finish_v(b, t - 1)
+
+        def finish_v(b, t0):
+            if t0 == 0:
+                v_grouped[b] = batch_pool.tile([P, H, PACK], BF16, name="v_grouped", align_bytes=64)
+            nc.vector.tensor_tensor(
+                out=v_grouped[b][:, :, t0 : t0 + 2],
+                in0=v_banks[b][:].rearrange("p t h -> p h t"),
+                in1=bv_bf[:].unsqueeze(2).to_broadcast([P, H, 2]),
+                op=ALU.add,
+            )
+            if t0 + 2 == BLOCKS:
+                v_codes[b] = batch_pool.tile([P, H], U32, name="v_codes", align_bytes=64)
+                v_scales[b] = batch_pool.tile([P, H], U8, name="v_scales", align_bytes=64)
+                nc.vector.quantize_mx(
+                    out=v_codes[b][:].bitcast(FP8X4),
+                    scales=v_scales[b][:],
+                    in_=v_grouped[b][:].rearrange("p h t -> p (h t)"),
+                )
+
+        row_max = keep.tile([P, UNITS], F32, name="row_max")
+        exp_bias = keep.tile([P, UNITS], F32, name="exp_bias")
+        row_sum = keep.tile([P, UNITS], F32, name="row_sum")
+        row_scale = keep.tile([P, UNITS], F32, name="row_scale")
+        z_tiles = {}
+        e_tiles = {}
+        e_grouped = {}
+        e_codes = {}
+        e_scales = {}
+
+        def logits(unit):
+            b, j = divmod(unit, BLOCKS)
+            qk = small_psum.tile([P, LK], F32, name="qk", tag="small")
+            for a in range(H_HALVES):
+                nc.tensor.matmul(
+                    out=qk[:],
+                    lhsT=qT[:, b, a, j * P : (j + 1) * P],
+                    rhs=kT[:, b, a, :],
+                    start=(a == 0),
+                    stop=(a == H_HALVES - 1),
+                )
+            z16 = stage.tile([P, LK], F32, name="z16")
+            nc.vector.scalar_tensor_tensor(
+                out=z16[:],
+                in0=log_pi[:, unit, :],
+                scalar=gamma16[:, 0:1],
+                in1=qk[:],
+                op0=ALU.mult,
+                op1=ALU.add,
+            )
+            nc.vector.reduce_max(out=row_max[:, unit : unit + 1], in_=z16[:], axis=AXIS.X)
+            nc.vector.tensor_scalar_mul(
+                out=exp_bias[:, unit : unit + 1],
+                in0=row_max[:, unit : unit + 1],
+                scalar1=-1.0 / SQRT_H,
+            )
+            z_tiles[unit] = z16
+
+        def exponentials(unit):
+            e_bf = stage.tile([P, LK], BF16, name="e_bf")
+            nc.scalar.activation(
+                out=e_bf[:],
+                in_=z_tiles[unit][:],
+                func=ACT.Exp,
+                bias=exp_bias[:, unit : unit + 1],
+                scale=1.0 / SQRT_H,
+                accum_out=row_sum[:, unit : unit + 1],
+            )
+            e_tiles[unit] = e_bf
+
+        def transpose_e(unit):
+            b, j = divmod(unit, BLOCKS)
+            if j == 0:
+                e_grouped[b] = batch_pool.tile(
+                    [P, BLOCKS, P, PACK], BF16, name="e_grouped", align_bytes=64
+                )
+            e_bf = e_tiles[unit]
+            bank = small_psum.tile([P, BLOCKS, P], BF16, name="eT", tag="small")
+            for t in range(BLOCKS):
+                nc.tensor.transpose(bank[:, t, :], e_bf[:, t * P : (t + 1) * P], ident_bf[:])
+            nc.vector.tensor_copy(out=e_grouped[b][:, j], in_=bank[:].rearrange("p t c -> p c t"))
+            if j == BLOCKS - 1:
+                e_codes[b] = batch_pool.tile([P, LQ], U32, name="e_codes", align_bytes=64)
+                e_scales[b] = batch_pool.tile([P, LQ], U8, name="e_scales", align_bytes=64)
+                nc.vector.quantize_mx(
+                    out=e_codes[b][:].bitcast(FP8X4),
+                    scales=e_scales[b][:],
+                    in_=e_grouped[b][:].rearrange("p j c t -> p (j c t)"),
+                )
+                units = slice(b * BLOCKS, (b + 1) * BLOCKS)
+                nc.vector.reciprocal(out=row_scale[:, units], in_=row_sum[:, units])
+
+        def attend(b):
+            o_sb = batch_pool.tile([P, BLOCKS, H], F32, name="o_sb")
+            for j0 in range(0, BLOCKS, 2):
+                bank = small_psum.tile([P, 2, H], F32, name="o_bank", tag="small")
+                for i in range(2):
+                    j = j0 + i
+                    nc.tensor.matmul_mx(
+                        out=bank[:, i, :],
+                        lhsT=e_codes[b][:, j * P : (j + 1) * P].bitcast(FP8X4),
+                        lhsT_scale=e_scales[b][:, j * P : (j + 1) * P],
+                        rhs=v_codes[b][:].bitcast(FP8X4),
+                        rhs_scale=v_scales[b][:],
+                        start=True,
+                        stop=True,
+                    )
+                unit = b * BLOCKS + j0
+                nc.vector.tensor_tensor(
+                    out=o_sb[:, j0 : j0 + 2, :],
+                    in0=bank[:],
+                    in1=row_scale[:, unit : unit + 2].unsqueeze(2).to_broadcast([P, 2, H]),
+                    op=ALU.mult,
+                )
+            nc.sync.dma_start(out=out[b].rearrange("(p j) h -> p j h", j=BLOCKS), in_=o_sb[:])
+
+        for r in range(ROUNDS + 2):
+            if r + X_BUFS - 1 < ROUNDS:
+                load_x(r + X_BUFS - 1)
+            if 1 <= r <= ROUNDS:
+                quantise_round(r - 1)
+            if r < ROUNDS:
+                transpose_round(r)
+            if 2 <= r < UNITS + 2:
+                transpose_e(r - 2)
+            if 1 <= r <= ROUNDS:
+                passes_round(r - 1)
+            if r < UNITS:
+                logits(r)
+            if 1 <= r <= UNITS:
+                exponentials(r - 1)
+            if r >= 2 and (r - 1) % ROUNDS_PER_BATCH == 0:
+                attend((r - 1) // ROUNDS_PER_BATCH - 1)

@@ -23,6 +23,7 @@ K_PASS = P * PACK
 GROUPS = DIN // K_PASS
 BLOCKS = LK // P
 UNITS = B * BLOCKS
+PAIRS = UNITS // 2
 H_HALVES = H // P
 
 ROUND_GROUPS = 8
@@ -33,7 +34,8 @@ ROUND_FEATURES = ROUND_GROUPS * K_PASS
 BANK_GROUPS = 2
 ROUND_BANKS = ROUND_GROUPS // BANK_GROUPS
 QUANT_GROUPS = 4
-X_BUFS = 8
+PASS_LAG = 2
+X_AHEAD = 5
 
 FLOPS = 2 * B * LK * DIN * H + 2 * B * LQ * LK * H + 2 * B * LQ * LK * H
 
@@ -45,40 +47,42 @@ def tile_pgwcrossattention_pa_k_kernel(
     with ExitStack() as ctx:
         ctx.enter_context(tc.manual_schedule())
         keep = ctx.enter_context(tc.tile_pool(name="keep", bufs=1))
-        x_pool = ctx.enter_context(tc.tile_pool(name="x", bufs=X_BUFS))
+        x_pool = ctx.enter_context(tc.tile_pool(name="x", bufs=X_AHEAD + 1))
         stage = ctx.enter_context(tc.tile_pool(name="stage", bufs=3))
+        code_pool = ctx.enter_context(tc.tile_pool(name="codes", bufs=PASS_LAG + 1))
         batch_pool = ctx.enter_context(tc.tile_pool(name="batch", bufs=B))
         xt_psum = ctx.enter_context(tc.psum_pool(name="xt_psum", bufs=ROUND_BANKS))
         v_psum = ctx.enter_context(tc.psum_pool(name="v_psum", bufs=2))
         small_psum = ctx.enter_context(tc.psum_pool(name="small_psum", bufs=2))
 
-        ident_f32 = keep.tile([P, P], F32, name="ident_f32")
-        make_identity(nc, ident_f32[:])
         ident_bf = keep.tile([P, P], BF16, name="ident_bf")
         make_identity(nc, ident_bf[:])
+        ident_f32 = keep.tile([P, P], F32, name="ident_f32")
+        make_identity(nc, ident_f32[:])
 
         w_scales = keep.tile([P, GROUPS, H], U8, name="w_scales", align_bytes=64)
         nc.vector.memset(w_scales[:].rearrange("p g n -> p (g n)").bitcast(I32), 0)
-        for first in range(2):
-            for row in range(4):
-                nc.sync.dma_start(
-                    out=w_scales[32 * first + row : P : 64].bitcast(I32),
-                    in_=Wv_scales[:, 4 * first + row : 16 : 8, :]
-                    .rearrange("g c n -> c g n")
-                    .bitcast(I32),
-                )
+        for row in range(4):
+            nc.gpsimd.dma_start(
+                out=w_scales[row:P:32].bitcast(F32),
+                in_=Wv_scales[:, row:16:4, :].rearrange("g s n -> s g n").bitcast(F32),
+            )
 
-        pi_sb = keep.tile([P, B, BLOCKS, LK], BF16, name="pi_sb")
-        nc.sync.dma_start(out=pi_sb[:], in_=pi_star.rearrange("b (p j) c -> p b j c", j=BLOCKS))
-        k_sb = keep.tile([P, B, BLOCKS, H], BF16, name="k_sb")
-        nc.sync.dma_start(out=k_sb[:], in_=k.rearrange("b (p t) h -> p b t h", t=BLOCKS))
-        q_sb = keep.tile([P, B, BLOCKS, H], BF16, name="q_sb")
-        nc.sync.dma_start(out=q_sb[:], in_=q.rearrange("b (p j) h -> p b j h", j=BLOCKS))
+        one = keep.tile([P, 1], F32, name="one")
+        nc.vector.memset(one[:], 1.0)
+        nc.scalar.activation(out=one[:], in_=one[:], func=ACT.Ln)
 
         gamma_bf = keep.tile([P, 1], BF16, name="gamma_bf")
         nc.scalar.dma_start(out=gamma_bf[:], in_=gamma.partition_broadcast(P))
         bv_bf = keep.tile([P, H], BF16, name="bv_bf")
         nc.scalar.dma_start(out=bv_bf[:], in_=bv.partition_broadcast(P))
+
+        k_sb = keep.tile([P, B, BLOCKS, H], BF16, name="k_sb")
+        nc.sync.dma_start(out=k_sb[:], in_=k.rearrange("b (p t) h -> p b t h", t=BLOCKS))
+        q_sb = keep.tile([P, B, BLOCKS, H], BF16, name="q_sb")
+        nc.sync.dma_start(out=q_sb[:], in_=q.rearrange("b (p j) h -> p b j h", j=BLOCKS))
+        pi_sb = keep.tile([P, B, BLOCKS, LK], BF16, name="pi_sb")
+        nc.sync.dma_start(out=pi_sb[:], in_=pi_star.rearrange("b (p j) c -> p b j c", j=BLOCKS))
 
         w_words = keep.tile([P, GROUPS, H], U32, name="w_words", align_bytes=64)
 
@@ -108,21 +112,8 @@ def tile_pgwcrossattention_pa_k_kernel(
         load_w(0)
         load_x(2)
         load_w(1)
-        for r in range(3, X_BUFS - 1):
+        for r in range(3, X_AHEAD):
             load_x(r)
-
-        gamma16 = keep.tile([P, 1], F32, name="gamma16")
-        nc.vector.tensor_scalar_mul(out=gamma16[:], in0=gamma_bf[:], scalar1=SQRT_H)
-
-        log_pi = keep.tile([P, UNITS, LK], F32, name="log_pi")
-        for unit in range(UNITS):
-            b, j = divmod(unit, BLOCKS)
-            nc.vector.tensor_scalar_max(
-                out=log_pi[:, unit, :].rearrange("p (t c) -> p t c", t=BLOCKS),
-                in0=pi_sb[:, b, j, :].rearrange("p (c t) -> p t c", t=BLOCKS),
-                scalar1=FLOOR,
-            )
-            nc.scalar.activation(out=log_pi[:, unit, :], in_=log_pi[:, unit, :], func=ACT.Ln)
 
         def transpose_rows(rows_sb, name):
             flipped = keep.tile([P, B, H_HALVES, LK], BF16, name=name)
@@ -133,20 +124,43 @@ def tile_pgwcrossattention_pa_k_kernel(
                         nc.tensor.transpose(
                             bank[:, a, i, :], rows_sb[:, b, i, a * P : (a + 1) * P], ident_bf[:]
                         )
-                nc.vector.tensor_copy(
-                    out=flipped[:, b], in_=bank[:].rearrange("p a i c -> p a (i c)")
-                )
+                nc.scalar.copy(out=flipped[:, b], in_=bank[:].rearrange("p a i c -> p a (i c)"))
             return flipped
 
         kT = transpose_rows(k_sb, "kT")
         qT = transpose_rows(q_sb, "qT")
 
+        gamma16 = keep.tile([P, 1], F32, name="gamma16")
+        nc.vector.tensor_scalar_mul(out=gamma16[:], in0=gamma_bf[:], scalar1=SQRT_H)
+
+        log_pi = keep.tile([P, UNITS, LK], F32, name="log_pi")
+        for unit in range(UNITS):
+            b, j = divmod(unit, BLOCKS)
+            nc.gpsimd.tensor_scalar(
+                out=log_pi[:, unit, :].rearrange("p (t c) -> p t c", t=BLOCKS),
+                in0=pi_sb[:, b, j, :].rearrange("p (c t) -> p t c", t=BLOCKS),
+                scalar1=FLOOR,
+                scalar2=0.0,
+                op0=ALU.max,
+                op1=ALU.add,
+            )
+            nc.scalar.activation(out=log_pi[:, unit, :], in_=log_pi[:, unit, :], func=ACT.Ln)
+
+        sorted_tiles = {}
         grouped_tiles = {}
         x_codes = {}
         x_scales = {}
 
+        def sort_words(r):
+            x_sorted = stage.tile([P, ROUND_GROUPS, 2, P], F32, name="x_sorted")
+            nc.vector.tensor_copy(
+                out=x_sorted[:],
+                in_=x_tiles[r][:].bitcast(F32).rearrange("p (g c u) -> p g u c", g=ROUND_GROUPS, u=2),
+            )
+            sorted_tiles[r] = x_sorted
+
         def transpose_round(r):
-            x_words = x_tiles[r][:].bitcast(F32)
+            x_sorted = sorted_tiles[r]
             grouped = stage.tile([P, ROUND_GROUPS * P * PACK], BF16, name="grouped", align_bytes=64)
             grouped_words = grouped[:].bitcast(F32).rearrange(
                 "p (a g c u) -> p a g c u", a=ROUND_BANKS, g=BANK_GROUPS, u=2
@@ -154,12 +168,9 @@ def tile_pgwcrossattention_pa_k_kernel(
             for a in range(ROUND_BANKS):
                 bank = xt_psum.tile([P, BANK_GROUPS, 2, P], F32, name="xt_bank", tag="xt")
                 for g in range(BANK_GROUPS):
-                    first_word = (a * BANK_GROUPS + g) * (K_PASS // 2)
                     for u in range(2):
                         nc.tensor.transpose(
-                            bank[:, g, u, :],
-                            x_words[:, first_word + u : first_word + K_PASS // 2 : 2],
-                            ident_f32[:],
+                            bank[:, g, u, :], x_sorted[:, a * BANK_GROUPS + g, u, :], ident_f32[:]
                         )
                 nc.scalar.copy(
                     out=grouped_words[:, a], in_=bank[:].rearrange("p g u c -> p g c u")
@@ -168,8 +179,8 @@ def tile_pgwcrossattention_pa_k_kernel(
 
         def quantise_round(r):
             grouped = grouped_tiles[r]
-            codes = stage.tile([P, ROUND_GROUPS * P], U32, name="codes", align_bytes=64)
-            scales = stage.tile([P, ROUND_GROUPS * P], U8, name="scales", align_bytes=64)
+            codes = code_pool.tile([P, ROUND_GROUPS * P], U32, name="codes", align_bytes=64)
+            scales = code_pool.tile([P, ROUND_GROUPS * P], U8, name="scales", align_bytes=64)
             width = QUANT_GROUPS * P
             for i in range(ROUND_GROUPS // QUANT_GROUPS):
                 nc.vector.quantize_mx(
@@ -190,14 +201,12 @@ def tile_pgwcrossattention_pa_k_kernel(
             b, t = divmod(block, BLOCKS)
             if part == 0 and t % 2 == 0:
                 v_banks[b] = v_psum.tile([P, 2, H], F32, name="v_bank")
-            codes = x_codes[r]
-            scales = x_scales[r]
             for i in range(ROUND_GROUPS):
                 g = part * ROUND_GROUPS + i
                 nc.tensor.matmul_mx(
                     out=v_banks[b][:, t % 2, :],
-                    lhsT=codes[:, i * P : (i + 1) * P].bitcast(FP8X4),
-                    lhsT_scale=scales[:, i * P : (i + 1) * P],
+                    lhsT=x_codes[r][:, i * P : (i + 1) * P].bitcast(FP8X4),
+                    lhsT_scale=x_scales[r][:, i * P : (i + 1) * P],
                     rhs=w_words[:, g, :].bitcast(FP8X4),
                     rhs_scale=w_scales[:, g, :],
                     start=(g == 0),
@@ -228,64 +237,75 @@ def tile_pgwcrossattention_pa_k_kernel(
         exp_bias = keep.tile([P, UNITS], F32, name="exp_bias")
         row_sum = keep.tile([P, UNITS], F32, name="row_sum")
         row_scale = keep.tile([P, UNITS], F32, name="row_scale")
+        qk_banks = {}
         z_tiles = {}
         e_tiles = {}
         e_grouped = {}
         e_codes = {}
         e_scales = {}
 
-        def logits(unit):
-            b, j = divmod(unit, BLOCKS)
-            qk = small_psum.tile([P, LK], F32, name="qk", tag="small")
-            for a in range(H_HALVES):
-                nc.tensor.matmul(
-                    out=qk[:],
-                    lhsT=qT[:, b, a, j * P : (j + 1) * P],
-                    rhs=kT[:, b, a, :],
-                    start=(a == 0),
-                    stop=(a == H_HALVES - 1),
+        def qk_matmuls(pair):
+            for unit in (2 * pair, 2 * pair + 1):
+                b, j = divmod(unit, BLOCKS)
+                qk = small_psum.tile([P, LK], F32, name="qk", tag="small")
+                for a in range(H_HALVES):
+                    nc.tensor.matmul(
+                        out=qk[:],
+                        lhsT=qT[:, b, a, j * P : (j + 1) * P],
+                        rhs=kT[:, b, a, :],
+                        start=(a == 0),
+                        stop=(a == H_HALVES - 1),
+                    )
+                qk_banks[unit] = qk
+
+        def add_prior(pair):
+            units = slice(2 * pair, 2 * pair + 2)
+            z16 = stage.tile([P, 2, LK], F32, name="z16")
+            for i in range(2):
+                nc.vector.scalar_tensor_tensor(
+                    out=z16[:, i, :],
+                    in0=log_pi[:, 2 * pair + i, :],
+                    scalar=gamma16[:, 0:1],
+                    in1=qk_banks[2 * pair + i][:],
+                    op0=ALU.mult,
+                    op1=ALU.add,
                 )
-            z16 = stage.tile([P, LK], F32, name="z16")
-            nc.vector.scalar_tensor_tensor(
-                out=z16[:],
-                in0=log_pi[:, unit, :],
-                scalar=gamma16[:, 0:1],
-                in1=qk[:],
-                op0=ALU.mult,
-                op1=ALU.add,
-            )
-            nc.vector.reduce_max(out=row_max[:, unit : unit + 1], in_=z16[:], axis=AXIS.X)
+            nc.vector.reduce_max(out=row_max[:, units], in_=z16[:], axis=AXIS.X)
             nc.vector.tensor_scalar_mul(
-                out=exp_bias[:, unit : unit + 1],
-                in0=row_max[:, unit : unit + 1],
-                scalar1=-1.0 / SQRT_H,
+                out=exp_bias[:, units], in0=row_max[:, units], scalar1=-1.0 / SQRT_H
             )
-            z_tiles[unit] = z16
+            z_tiles[pair] = z16
 
-        def exponentials(unit):
-            e_bf = stage.tile([P, LK], BF16, name="e_bf")
-            nc.scalar.activation(
-                out=e_bf[:],
-                in_=z_tiles[unit][:],
-                func=ACT.Exp,
-                bias=exp_bias[:, unit : unit + 1],
-                scale=1.0 / SQRT_H,
-                accum_out=row_sum[:, unit : unit + 1],
-            )
-            e_tiles[unit] = e_bf
+        def exponentials(pair):
+            e_bf = stage.tile([P, 2, LK], BF16, name="e_bf")
+            for i in range(2):
+                unit = 2 * pair + i
+                nc.scalar.activation(
+                    out=e_bf[:, i, :],
+                    in_=z_tiles[pair][:, i, :],
+                    func=ACT.Exp,
+                    bias=exp_bias[:, unit : unit + 1],
+                    scale=1.0 / SQRT_H,
+                    accum_out=row_sum[:, unit : unit + 1],
+                )
+            e_tiles[pair] = e_bf
 
-        def transpose_e(unit):
-            b, j = divmod(unit, BLOCKS)
-            if j == 0:
+        def transpose_e(pair):
+            b, j0 = divmod(2 * pair, BLOCKS)
+            if j0 == 0:
                 e_grouped[b] = batch_pool.tile(
                     [P, BLOCKS, P, PACK], BF16, name="e_grouped", align_bytes=64
                 )
-            e_bf = e_tiles[unit]
-            bank = small_psum.tile([P, BLOCKS, P], BF16, name="eT", tag="small")
-            for t in range(BLOCKS):
-                nc.tensor.transpose(bank[:, t, :], e_bf[:, t * P : (t + 1) * P], ident_bf[:])
-            nc.vector.tensor_copy(out=e_grouped[b][:, j], in_=bank[:].rearrange("p t c -> p c t"))
-            if j == BLOCKS - 1:
+            bank = small_psum.tile([P, 2, BLOCKS, P], BF16, name="eT", tag="small")
+            for i in range(2):
+                for t in range(BLOCKS):
+                    nc.tensor.transpose(
+                        bank[:, i, t, :], e_tiles[pair][:, i, t * P : (t + 1) * P], ident_bf[:]
+                    )
+            nc.scalar.copy(
+                out=e_grouped[b][:, j0 : j0 + 2], in_=bank[:].rearrange("p i t c -> p i c t")
+            )
+            if j0 + 2 == BLOCKS:
                 e_codes[b] = batch_pool.tile([P, LQ], U32, name="e_codes", align_bytes=64)
                 e_scales[b] = batch_pool.tile([P, LQ], U8, name="e_scales", align_bytes=64)
                 nc.vector.quantize_mx(
@@ -312,28 +332,47 @@ def tile_pgwcrossattention_pa_k_kernel(
                         stop=True,
                     )
                 unit = b * BLOCKS + j0
-                nc.vector.tensor_tensor(
-                    out=o_sb[:, j0 : j0 + 2, :],
-                    in0=bank[:],
-                    in1=row_scale[:, unit : unit + 2].unsqueeze(2).to_broadcast([P, 2, H]),
-                    op=ALU.mult,
+                if j0 == 0:
+                    nc.vector.tensor_tensor(
+                        out=o_sb[:, j0 : j0 + 2, :],
+                        in0=bank[:],
+                        in1=row_scale[:, unit : unit + 2].unsqueeze(2).to_broadcast([P, 2, H]),
+                        op=ALU.mult,
+                    )
+                else:
+                    for i in range(2):
+                        nc.scalar.activation(
+                            out=o_sb[:, j0 + i, :],
+                            in_=bank[:, i, :],
+                            func=ACT.Copy,
+                            scale=row_scale[:, unit + i : unit + i + 1],
+                        )
+                nc.sync.dma_start(
+                    out=out[b].rearrange("(p j) h -> p j h", j=BLOCKS)[:, j0 : j0 + 2, :],
+                    in_=o_sb[:, j0 : j0 + 2, :],
                 )
-            nc.sync.dma_start(out=out[b].rearrange("(p j) h -> p j h", j=BLOCKS), in_=o_sb[:])
 
-        for r in range(ROUNDS + 2):
-            if r + X_BUFS - 1 < ROUNDS:
-                load_x(r + X_BUFS - 1)
+        qk_matmuls(0)
+        sort_words(0)
+        for r in range(ROUNDS + PASS_LAG):
+            if r + X_AHEAD < ROUNDS:
+                load_x(r + X_AHEAD)
+            if r < PAIRS:
+                add_prior(r)
             if 1 <= r <= ROUNDS:
                 quantise_round(r - 1)
+            if r + 1 < ROUNDS:
+                sort_words(r + 1)
             if r < ROUNDS:
                 transpose_round(r)
-            if 2 <= r < UNITS + 2:
+            if 2 <= r < PAIRS + 2:
                 transpose_e(r - 2)
-            if 1 <= r <= ROUNDS:
-                passes_round(r - 1)
-            if r < UNITS:
-                logits(r)
-            if 1 <= r <= UNITS:
-                exponentials(r - 1)
-            if r >= 2 and (r - 1) % ROUNDS_PER_BATCH == 0:
-                attend((r - 1) // ROUNDS_PER_BATCH - 1)
+            if r >= PASS_LAG:
+                passes_round(r - PASS_LAG)
+            if r + 1 < PAIRS:
+                qk_matmuls(r + 1)
+            if r < PAIRS:
+                exponentials(r)
+            if r == ROUNDS_PER_BATCH + PASS_LAG:
+                attend(0)
+        attend(1)

@@ -62,11 +62,13 @@ def tile_pgwcrossattention_pa_k_kernel(
 
         w_scales = keep.tile([P, GROUPS, H], U8, name="w_scales", align_bytes=64)
         nc.vector.memset(w_scales[:].rearrange("p g n -> p (g n)").bitcast(I32), 0)
-        for row in range(4):
-            nc.gpsimd.dma_start(
-                out=w_scales[row:P:32].bitcast(F32),
-                in_=Wv_scales[:, row:16:4, :].rearrange("g s n -> s g n").bitcast(F32),
-            )
+
+        def load_w_scales():
+            for row in range(4):
+                nc.sync.dma_start(
+                    out=w_scales[row:P:32].bitcast(I32),
+                    in_=Wv_scales[:, row:16:4, :].rearrange("g s n -> s g n").bitcast(I32),
+                )
 
         one = keep.tile([P, 1], F32, name="one")
         nc.vector.memset(one[:], 1.0)
@@ -77,12 +79,12 @@ def tile_pgwcrossattention_pa_k_kernel(
         bv_bf = keep.tile([P, H], BF16, name="bv_bf")
         nc.scalar.dma_start(out=bv_bf[:], in_=bv.partition_broadcast(P))
 
+        pi_sb = keep.tile([P, B, BLOCKS, LK], BF16, name="pi_sb")
+        nc.sync.dma_start(out=pi_sb[:], in_=pi_star.rearrange("b (p j) c -> p b j c", j=BLOCKS))
         k_sb = keep.tile([P, B, BLOCKS, H], BF16, name="k_sb")
         nc.sync.dma_start(out=k_sb[:], in_=k.rearrange("b (p t) h -> p b t h", t=BLOCKS))
         q_sb = keep.tile([P, B, BLOCKS, H], BF16, name="q_sb")
         nc.sync.dma_start(out=q_sb[:], in_=q.rearrange("b (p j) h -> p b j h", j=BLOCKS))
-        pi_sb = keep.tile([P, B, BLOCKS, LK], BF16, name="pi_sb")
-        nc.sync.dma_start(out=pi_sb[:], in_=pi_star.rearrange("b (p j) c -> p b j c", j=BLOCKS))
 
         w_words = keep.tile([P, GROUPS, H], U32, name="w_words", align_bytes=64)
 
@@ -108,12 +110,26 @@ def tile_pgwcrossattention_pa_k_kernel(
             x_tiles[r] = x_sb
 
         load_x(0)
+        load_w_scales()
         load_x(1)
         load_w(0)
         load_x(2)
         load_w(1)
         for r in range(3, X_AHEAD):
             load_x(r)
+
+        gamma16 = keep.tile([P, 1], F32, name="gamma16")
+        nc.vector.tensor_scalar_mul(out=gamma16[:], in0=gamma_bf[:], scalar1=SQRT_H)
+
+        log_pi = keep.tile([P, UNITS, LK], F32, name="log_pi")
+        for unit in range(UNITS):
+            b, j = divmod(unit, BLOCKS)
+            nc.vector.tensor_scalar_max(
+                out=log_pi[:, unit, :].rearrange("p (t c) -> p t c", t=BLOCKS),
+                in0=pi_sb[:, b, j, :].rearrange("p (c t) -> p t c", t=BLOCKS),
+                scalar1=FLOOR,
+            )
+            nc.scalar.activation(out=log_pi[:, unit, :], in_=log_pi[:, unit, :], func=ACT.Ln)
 
         def transpose_rows(rows_sb, name):
             flipped = keep.tile([P, B, H_HALVES, LK], BF16, name=name)
@@ -124,27 +140,13 @@ def tile_pgwcrossattention_pa_k_kernel(
                         nc.tensor.transpose(
                             bank[:, a, i, :], rows_sb[:, b, i, a * P : (a + 1) * P], ident_bf[:]
                         )
-                nc.scalar.copy(out=flipped[:, b], in_=bank[:].rearrange("p a i c -> p a (i c)"))
+                nc.vector.tensor_copy(
+                    out=flipped[:, b], in_=bank[:].rearrange("p a i c -> p a (i c)")
+                )
             return flipped
 
         kT = transpose_rows(k_sb, "kT")
         qT = transpose_rows(q_sb, "qT")
-
-        gamma16 = keep.tile([P, 1], F32, name="gamma16")
-        nc.vector.tensor_scalar_mul(out=gamma16[:], in0=gamma_bf[:], scalar1=SQRT_H)
-
-        log_pi = keep.tile([P, UNITS, LK], F32, name="log_pi")
-        for unit in range(UNITS):
-            b, j = divmod(unit, BLOCKS)
-            nc.gpsimd.tensor_scalar(
-                out=log_pi[:, unit, :].rearrange("p (t c) -> p t c", t=BLOCKS),
-                in0=pi_sb[:, b, j, :].rearrange("p (c t) -> p t c", t=BLOCKS),
-                scalar1=FLOOR,
-                scalar2=0.0,
-                op0=ALU.max,
-                op1=ALU.add,
-            )
-            nc.scalar.activation(out=log_pi[:, unit, :], in_=log_pi[:, unit, :], func=ACT.Ln)
 
         sorted_tiles = {}
         grouped_tiles = {}
@@ -212,10 +214,13 @@ def tile_pgwcrossattention_pa_k_kernel(
                     start=(g == 0),
                     stop=(g == GROUPS - 1),
                 )
-            if part == ROUNDS_PER_BLOCK - 1 and t % 2 == 1:
-                finish_v(b, t - 1)
 
-        def finish_v(b, t0):
+        def finish_v(r):
+            block, part = divmod(r, ROUNDS_PER_BLOCK)
+            b, t = divmod(block, BLOCKS)
+            if part != ROUNDS_PER_BLOCK - 1 or t % 2 == 0:
+                return
+            t0 = t - 1
             if t0 == 0:
                 v_grouped[b] = batch_pool.tile([P, H, PACK], BF16, name="v_grouped", align_bytes=64)
             nc.vector.tensor_tensor(
@@ -305,16 +310,20 @@ def tile_pgwcrossattention_pa_k_kernel(
             nc.scalar.copy(
                 out=e_grouped[b][:, j0 : j0 + 2], in_=bank[:].rearrange("p i t c -> p i c t")
             )
-            if j0 + 2 == BLOCKS:
-                e_codes[b] = batch_pool.tile([P, LQ], U32, name="e_codes", align_bytes=64)
-                e_scales[b] = batch_pool.tile([P, LQ], U8, name="e_scales", align_bytes=64)
-                nc.vector.quantize_mx(
-                    out=e_codes[b][:].bitcast(FP8X4),
-                    scales=e_scales[b][:],
-                    in_=e_grouped[b][:].rearrange("p j c t -> p (j c t)"),
-                )
-                units = slice(b * BLOCKS, (b + 1) * BLOCKS)
-                nc.vector.reciprocal(out=row_scale[:, units], in_=row_sum[:, units])
+
+        def quantise_e(pair):
+            b, j0 = divmod(2 * pair, BLOCKS)
+            if j0 + 2 != BLOCKS:
+                return
+            e_codes[b] = batch_pool.tile([P, LQ], U32, name="e_codes", align_bytes=64)
+            e_scales[b] = batch_pool.tile([P, LQ], U8, name="e_scales", align_bytes=64)
+            nc.vector.quantize_mx(
+                out=e_codes[b][:].bitcast(FP8X4),
+                scales=e_scales[b][:],
+                in_=e_grouped[b][:].rearrange("p j c t -> p (j c t)"),
+            )
+            units = slice(b * BLOCKS, (b + 1) * BLOCKS)
+            nc.vector.reciprocal(out=row_scale[:, units], in_=row_sum[:, units])
 
         def attend(b):
             o_sb = batch_pool.tile([P, BLOCKS, H], F32, name="o_sb")
@@ -363,6 +372,10 @@ def tile_pgwcrossattention_pa_k_kernel(
                 quantise_round(r - 1)
             if r + 1 < ROUNDS:
                 sort_words(r + 1)
+            if r >= PASS_LAG + 1:
+                finish_v(r - PASS_LAG - 1)
+            if 4 <= r < PAIRS + 4:
+                quantise_e(r - 4)
             if r < ROUNDS:
                 transpose_round(r)
             if 2 <= r < PAIRS + 2:
@@ -373,6 +386,7 @@ def tile_pgwcrossattention_pa_k_kernel(
                 qk_matmuls(r + 1)
             if r < PAIRS:
                 exponentials(r)
-            if r == ROUNDS_PER_BATCH + PASS_LAG:
+            if r == ROUNDS_PER_BATCH + PASS_LAG + 1:
                 attend(0)
+        finish_v(ROUNDS - 1)
         attend(1)

@@ -36,6 +36,7 @@ ROUND_BANKS = ROUND_GROUPS // BANK_GROUPS
 QUANT_GROUPS = 4
 PASS_LAG = 2
 X_AHEAD = 5
+SORT_FROM = 4
 
 FLOPS = 2 * B * LK * DIN * H + 2 * B * LQ * LK * H + 2 * B * LQ * LK * H
 
@@ -148,21 +149,24 @@ def tile_pgwcrossattention_pa_k_kernel(
         kT = transpose_rows(k_sb, "kT")
         qT = transpose_rows(q_sb, "qT")
 
-        sorted_tiles = {}
+        word_views = {}
         grouped_tiles = {}
         x_codes = {}
         x_scales = {}
 
         def sort_words(r):
-            x_sorted = stage.tile([P, ROUND_GROUPS, 2, P], F32, name="x_sorted")
-            nc.vector.tensor_copy(
-                out=x_sorted[:],
-                in_=x_tiles[r][:].bitcast(F32).rearrange("p (g c u) -> p g u c", g=ROUND_GROUPS, u=2),
+            as_loaded = x_tiles[r][:].bitcast(F32).rearrange(
+                "p (g c u) -> p g u c", g=ROUND_GROUPS, u=2
             )
-            sorted_tiles[r] = x_sorted
+            if r < SORT_FROM:
+                word_views[r] = as_loaded
+                return
+            x_sorted = stage.tile([P, ROUND_GROUPS, 2, P], F32, name="x_sorted")
+            nc.vector.tensor_copy(out=x_sorted[:], in_=as_loaded)
+            word_views[r] = x_sorted[:]
 
         def transpose_round(r):
-            x_sorted = sorted_tiles[r]
+            words = word_views[r]
             grouped = stage.tile([P, ROUND_GROUPS * P * PACK], BF16, name="grouped", align_bytes=64)
             grouped_words = grouped[:].bitcast(F32).rearrange(
                 "p (a g c u) -> p a g c u", a=ROUND_BANKS, g=BANK_GROUPS, u=2
@@ -172,7 +176,7 @@ def tile_pgwcrossattention_pa_k_kernel(
                 for g in range(BANK_GROUPS):
                     for u in range(2):
                         nc.tensor.transpose(
-                            bank[:, g, u, :], x_sorted[:, a * BANK_GROUPS + g, u, :], ident_f32[:]
+                            bank[:, g, u, :], words[:, a * BANK_GROUPS + g, u, :], ident_f32[:]
                         )
                 nc.scalar.copy(
                     out=grouped_words[:, a], in_=bank[:].rearrange("p g u c -> p g c u")
@@ -264,7 +268,6 @@ def tile_pgwcrossattention_pa_k_kernel(
                 qk_banks[unit] = qk
 
         def add_prior(pair):
-            units = slice(2 * pair, 2 * pair + 2)
             z16 = stage.tile([P, 2, LK], F32, name="z16")
             for i in range(2):
                 nc.vector.scalar_tensor_tensor(
@@ -275,11 +278,17 @@ def tile_pgwcrossattention_pa_k_kernel(
                     op0=ALU.mult,
                     op1=ALU.add,
                 )
-            nc.vector.reduce_max(out=row_max[:, units], in_=z16[:], axis=AXIS.X)
+            z_tiles[pair] = z16
+
+        def row_maxima(pair):
+            units = slice(2 * pair, 2 * pair + 2)
+            nc.vector.reduce_max(out=row_max[:, units], in_=z_tiles[pair][:], axis=AXIS.X)
+
+        def exp_biases(pair):
+            units = slice(2 * pair, 2 * pair + 2)
             nc.vector.tensor_scalar_mul(
                 out=exp_bias[:, units], in0=row_max[:, units], scalar1=-1.0 / SQRT_H
             )
-            z_tiles[pair] = z16
 
         def exponentials(pair):
             e_bf = stage.tile([P, 2, LK], BF16, name="e_bf")
@@ -370,8 +379,12 @@ def tile_pgwcrossattention_pa_k_kernel(
                 add_prior(r)
             if 1 <= r <= ROUNDS:
                 quantise_round(r - 1)
+            if r < PAIRS:
+                row_maxima(r)
             if r + 1 < ROUNDS:
                 sort_words(r + 1)
+            if r < PAIRS:
+                exp_biases(r)
             if r >= PASS_LAG + 1:
                 finish_v(r - PASS_LAG - 1)
             if 4 <= r < PAIRS + 4:

@@ -131,6 +131,7 @@ def tile_pgwcrossattention_pa_k_kernel(
                 scalar1=FLOOR,
             )
             nc.scalar.activation(out=log_pi[:, unit, :], in_=log_pi[:, unit, :], func=ACT.Ln)
+        nc.scalar.activation(out=one[:], in_=one[:], func=ACT.Exp)
 
         def transpose_rows(rows_sb, name):
             flipped = keep.tile([P, B, H_HALVES, LK], BF16, name=name)
@@ -178,9 +179,14 @@ def tile_pgwcrossattention_pa_k_kernel(
                         nc.tensor.transpose(
                             bank[:, g, u, :], words[:, a * BANK_GROUPS + g, u, :], ident_f32[:]
                         )
-                nc.scalar.copy(
-                    out=grouped_words[:, a], in_=bank[:].rearrange("p g u c -> p g c u")
-                )
+                if r < SORT_FROM and a == ROUND_BANKS - 1:
+                    nc.vector.tensor_copy(
+                        out=grouped_words[:, a], in_=bank[:].rearrange("p g u c -> p g c u")
+                    )
+                else:
+                    nc.scalar.copy(
+                        out=grouped_words[:, a], in_=bank[:].rearrange("p g u c -> p g c u")
+                    )
             grouped_tiles[r] = grouped
 
         def quantise_round(r):

@@ -33,7 +33,6 @@ ROUNDS_PER_BATCH = ROUNDS // B
 ROUND_FEATURES = ROUND_GROUPS * K_PASS
 BANK_GROUPS = 2
 ROUND_BANKS = ROUND_GROUPS // BANK_GROUPS
-QUANT_GROUPS = 4
 PASS_LAG = 2
 X_AHEAD = 5
 SORT_FROM = 4
@@ -77,8 +76,6 @@ def tile_pgwcrossattention_pa_k_kernel(
 
         gamma_bf = keep.tile([P, 1], BF16, name="gamma_bf")
         nc.scalar.dma_start(out=gamma_bf[:], in_=gamma.partition_broadcast(P))
-        bv_bf = keep.tile([P, H], BF16, name="bv_bf")
-        nc.scalar.dma_start(out=bv_bf[:], in_=bv.partition_broadcast(P))
 
         pi_sb = keep.tile([P, B, BLOCKS, LK], BF16, name="pi_sb")
         nc.sync.dma_start(out=pi_sb[:], in_=pi_star.rearrange("b (p j) c -> p b j c", j=BLOCKS))
@@ -118,20 +115,22 @@ def tile_pgwcrossattention_pa_k_kernel(
         load_w(1)
         for r in range(3, X_AHEAD):
             load_x(r)
+        bv_bf = keep.tile([P, H], BF16, name="bv_bf")
+        nc.sync.dma_start(out=bv_bf[:], in_=bv.partition_broadcast(P))
+
+        log_pi = keep.tile([P, UNITS, LK], F32, name="log_pi")
+        for b in range(B):
+            units = slice(b * BLOCKS, (b + 1) * BLOCKS)
+            nc.vector.tensor_scalar_max(
+                out=log_pi[:, units, :].rearrange("p j (t c) -> p j t c", t=BLOCKS),
+                in0=pi_sb[:, b].rearrange("p j (c t) -> p j t c", t=BLOCKS),
+                scalar1=FLOOR,
+            )
+            nc.scalar.activation(out=log_pi[:, units, :], in_=log_pi[:, units, :], func=ACT.Ln)
+        nc.scalar.activation(out=one[:], in_=one[:], func=ACT.Exp)
 
         gamma16 = keep.tile([P, 1], F32, name="gamma16")
         nc.vector.tensor_scalar_mul(out=gamma16[:], in0=gamma_bf[:], scalar1=SQRT_H)
-
-        log_pi = keep.tile([P, UNITS, LK], F32, name="log_pi")
-        for unit in range(UNITS):
-            b, j = divmod(unit, BLOCKS)
-            nc.vector.tensor_scalar_max(
-                out=log_pi[:, unit, :].rearrange("p (t c) -> p t c", t=BLOCKS),
-                in0=pi_sb[:, b, j, :].rearrange("p (c t) -> p t c", t=BLOCKS),
-                scalar1=FLOOR,
-            )
-            nc.scalar.activation(out=log_pi[:, unit, :], in_=log_pi[:, unit, :], func=ACT.Ln)
-        nc.scalar.activation(out=one[:], in_=one[:], func=ACT.Exp)
 
         def transpose_rows(rows_sb, name):
             flipped = keep.tile([P, B, H_HALVES, LK], BF16, name=name)
@@ -193,13 +192,7 @@ def tile_pgwcrossattention_pa_k_kernel(
             grouped = grouped_tiles[r]
             codes = code_pool.tile([P, ROUND_GROUPS * P], U32, name="codes", align_bytes=64)
             scales = code_pool.tile([P, ROUND_GROUPS * P], U8, name="scales", align_bytes=64)
-            width = QUANT_GROUPS * P
-            for i in range(ROUND_GROUPS // QUANT_GROUPS):
-                nc.vector.quantize_mx(
-                    out=codes[:, i * width : (i + 1) * width].bitcast(FP8X4),
-                    scales=scales[:, i * width : (i + 1) * width],
-                    in_=grouped[:, i * width * PACK : (i + 1) * width * PACK],
-                )
+            nc.vector.quantize_mx(out=codes[:].bitcast(FP8X4), scales=scales[:], in_=grouped[:])
             x_codes[r] = codes
             x_scales[r] = scales
 

@@ -74,15 +74,19 @@ def tile_pgwcrossattention_pa_k_kernel(
         nc.vector.memset(one[:], 1.0)
         nc.scalar.activation(out=one[:], in_=one[:], func=ACT.Ln)
 
-        gamma_bf = keep.tile([P, 1], BF16, name="gamma_bf")
-        nc.scalar.dma_start(out=gamma_bf[:], in_=gamma.partition_broadcast(P))
+        rows = keep.tile([P, H + 2], BF16, name="rows")
+        nc.vector.memset(rows[:], 0.0)
+        ones = keep.tile([P, P], BF16, name="ones")
+        nc.vector.memset(ones[:], 1.0)
+        nc.scalar.dma_start(out=rows[0:1, H : H + 1], in_=gamma.rearrange("(a n) -> a n", a=1))
+        nc.scalar.dma_start(out=rows[0:1, 0:H], in_=bv.rearrange("(a n) -> a n", a=1))
 
         pi_sb = keep.tile([P, B, BLOCKS, LK], BF16, name="pi_sb")
-        nc.sync.dma_start(out=pi_sb[:], in_=pi_star.rearrange("b (p j) c -> p b j c", j=BLOCKS))
         k_sb = keep.tile([P, B, BLOCKS, H], BF16, name="k_sb")
         nc.sync.dma_start(out=k_sb[:], in_=k.rearrange("b (p t) h -> p b t h", t=BLOCKS))
         q_sb = keep.tile([P, B, BLOCKS, H], BF16, name="q_sb")
         nc.sync.dma_start(out=q_sb[:], in_=q.rearrange("b (p j) h -> p b j h", j=BLOCKS))
+        nc.sync.dma_start(out=pi_sb[:], in_=pi_star.rearrange("b (p j) c -> p b j c", j=BLOCKS))
 
         w_words = keep.tile([P, GROUPS, H], U32, name="w_words", align_bytes=64)
 
@@ -115,8 +119,23 @@ def tile_pgwcrossattention_pa_k_kernel(
         load_w(1)
         for r in range(3, X_AHEAD):
             load_x(r)
-        bv_bf = keep.tile([P, H], BF16, name="bv_bf")
-        nc.sync.dma_start(out=bv_bf[:], in_=bv.partition_broadcast(P))
+
+        def transpose_rows(rows_sb, name, factor):
+            flipped = keep.tile([P, B, H_HALVES, LK], BF16, name=name)
+            for b in range(B):
+                bank = xt_psum.tile([P, H_HALVES, BLOCKS, P], BF16, name="qk_bank", tag="xt")
+                for a in range(H_HALVES):
+                    for i in range(BLOCKS):
+                        nc.tensor.transpose(
+                            bank[:, a, i, :], rows_sb[:, b, i, a * P : (a + 1) * P], ident_bf[:]
+                        )
+                nc.vector.tensor_scalar_mul(
+                    out=flipped[:, b], in0=bank[:].rearrange("p a i c -> p a (i c)"), scalar1=factor
+                )
+            return flipped
+
+        kT = transpose_rows(k_sb, "kT", 1.0)
+        qT = transpose_rows(q_sb, "qT", 1.0 / SQRT_H)
 
         log_pi = keep.tile([P, UNITS, LK], F32, name="log_pi")
         for b in range(B):
@@ -129,25 +148,12 @@ def tile_pgwcrossattention_pa_k_kernel(
             nc.scalar.activation(out=log_pi[:, units, :], in_=log_pi[:, units, :], func=ACT.Ln)
         nc.scalar.activation(out=one[:], in_=one[:], func=ACT.Exp)
 
-        gamma16 = keep.tile([P, 1], F32, name="gamma16")
-        nc.vector.tensor_scalar_mul(out=gamma16[:], in0=gamma_bf[:], scalar1=SQRT_H)
-
-        def transpose_rows(rows_sb, name):
-            flipped = keep.tile([P, B, H_HALVES, LK], BF16, name=name)
-            for b in range(B):
-                bank = xt_psum.tile([P, H_HALVES, BLOCKS, P], BF16, name="qk_bank", tag="xt")
-                for a in range(H_HALVES):
-                    for i in range(BLOCKS):
-                        nc.tensor.transpose(
-                            bank[:, a, i, :], rows_sb[:, b, i, a * P : (a + 1) * P], ident_bf[:]
-                        )
-                nc.vector.tensor_copy(
-                    out=flipped[:, b], in_=bank[:].rearrange("p a i c -> p a (i c)")
-                )
-            return flipped
-
-        kT = transpose_rows(k_sb, "kT")
-        qT = transpose_rows(q_sb, "qT")
+        spread = keep.tile([P, H + 2], F32, name="spread")
+        spread_bank = small_psum.tile([P, H + 2], F32, name="spread_bank", tag="small")
+        nc.tensor.matmul(out=spread_bank[:], lhsT=ones[:], rhs=rows[:], start=True, stop=True)
+        nc.vector.tensor_copy(out=spread[:], in_=spread_bank[:])
+        bv_f32 = spread[:, 0:H]
+        gamma_f32 = spread[:, H : H + 1]
 
         word_views = {}
         grouped_tiles = {}
@@ -229,7 +235,7 @@ def tile_pgwcrossattention_pa_k_kernel(
             nc.vector.tensor_tensor(
                 out=v_grouped[b][:, :, t0 : t0 + 2],
                 in0=v_banks[b][:].rearrange("p t h -> p h t"),
-                in1=bv_bf[:].unsqueeze(2).to_broadcast([P, H, 2]),
+                in1=bv_f32.unsqueeze(2).to_broadcast([P, H, 2]),
                 op=ALU.add,
             )
             if t0 + 2 == BLOCKS:
@@ -241,7 +247,6 @@ def tile_pgwcrossattention_pa_k_kernel(
                     in_=v_grouped[b][:].rearrange("p h t -> p (h t)"),
                 )
 
-        row_max = keep.tile([P, UNITS], F32, name="row_max")
         exp_bias = keep.tile([P, UNITS], F32, name="exp_bias")
         row_sum = keep.tile([P, UNITS], F32, name="row_sum")
         row_scale = keep.tile([P, UNITS], F32, name="row_scale")
@@ -267,26 +272,22 @@ def tile_pgwcrossattention_pa_k_kernel(
                 qk_banks[unit] = qk
 
         def add_prior(pair):
-            z16 = stage.tile([P, 2, LK], F32, name="z16")
+            z = stage.tile([P, 2, LK], F32, name="z")
             for i in range(2):
                 nc.vector.scalar_tensor_tensor(
-                    out=z16[:, i, :],
+                    out=z[:, i, :],
                     in0=log_pi[:, 2 * pair + i, :],
-                    scalar=gamma16[:, 0:1],
+                    scalar=gamma_f32,
                     in1=qk_banks[2 * pair + i][:],
                     op0=ALU.mult,
                     op1=ALU.add,
                 )
-            z_tiles[pair] = z16
+            z_tiles[pair] = z
 
         def row_maxima(pair):
             units = slice(2 * pair, 2 * pair + 2)
-            nc.vector.reduce_max(out=row_max[:, units], in_=z_tiles[pair][:], axis=AXIS.X)
-
-        def exp_biases(pair):
-            units = slice(2 * pair, 2 * pair + 2)
-            nc.vector.tensor_scalar_mul(
-                out=exp_bias[:, units], in0=row_max[:, units], scalar1=-1.0 / SQRT_H
+            nc.vector.reduce_max(
+                out=exp_bias[:, units], in_=z_tiles[pair][:], axis=AXIS.X, negate=True
             )
 
         def exponentials(pair):
@@ -294,11 +295,11 @@ def tile_pgwcrossattention_pa_k_kernel(
             for i in range(2):
                 unit = 2 * pair + i
                 nc.scalar.activation(
-                    out=e_bf[:, i, :],
-                    in_=z_tiles[pair][:, i, :],
+                    out=e_bf[:, i, :].rearrange("p (u c e) -> p u c e", u=2, e=2),
+                    in_=z_tiles[pair][:, i, :].rearrange("p (u e c) -> p u c e", u=2, e=2),
                     func=ACT.Exp,
                     bias=exp_bias[:, unit : unit + 1],
-                    scale=1.0 / SQRT_H,
+                    scale=1.0,
                     accum_out=row_sum[:, unit : unit + 1],
                 )
             e_tiles[pair] = e_bf
@@ -309,14 +310,17 @@ def tile_pgwcrossattention_pa_k_kernel(
                 e_grouped[b] = batch_pool.tile(
                     [P, BLOCKS, P, PACK], BF16, name="e_grouped", align_bytes=64
                 )
-            bank = small_psum.tile([P, 2, BLOCKS, P], BF16, name="eT", tag="small")
+            bank = small_psum.tile([P, 2, 2, P], F32, name="eT", tag="small")
             for i in range(2):
-                for t in range(BLOCKS):
+                words = e_tiles[pair][:, i, :].bitcast(F32)
+                for u in range(2):
                     nc.tensor.transpose(
-                        bank[:, i, t, :], e_tiles[pair][:, i, t * P : (t + 1) * P], ident_bf[:]
+                        bank[:, i, u, :], words[:, u * P : (u + 1) * P], ident_f32[:]
                     )
             nc.scalar.copy(
-                out=e_grouped[b][:, j0 : j0 + 2], in_=bank[:].rearrange("p i t c -> p i c t")
+                out=e_grouped[b][:].rearrange("p j c t -> p j (c t)").bitcast(F32)
+                .rearrange("p j (c u) -> p j c u", u=2)[:, j0 : j0 + 2],
+                in_=bank[:].rearrange("p i u c -> p i c u"),
             )
 
         def quantise_e(pair):
@@ -382,8 +386,6 @@ def tile_pgwcrossattention_pa_k_kernel(
                 row_maxima(r)
             if r + 1 < ROUNDS:
                 sort_words(r + 1)
-            if r < PAIRS:
-                exp_biases(r)
             if r >= PASS_LAG + 1:
                 finish_v(r - PASS_LAG - 1)
             if 4 <= r < PAIRS + 4:

@@ -78,8 +78,8 @@ def tile_pgwcrossattention_pa_k_kernel(
         nc.vector.memset(rows[:], 0.0)
         ones = keep.tile([P, P], BF16, name="ones")
         nc.vector.memset(ones[:], 1.0)
-        nc.scalar.dma_start(out=rows[0:1, H : H + 1], in_=gamma.rearrange("(a n) -> a n", a=1))
-        nc.scalar.dma_start(out=rows[0:1, 0:H], in_=bv.rearrange("(a n) -> a n", a=1))
+        nc.sync.dma_start(out=rows[0:1, H : H + 1], in_=gamma.rearrange("(a n) -> a n", a=1))
+        nc.sync.dma_start(out=rows[0:1, 0:H], in_=bv.rearrange("(a n) -> a n", a=1))
 
         pi_sb = keep.tile([P, B, BLOCKS, LK], BF16, name="pi_sb")
         k_sb = keep.tile([P, B, BLOCKS, H], BF16, name="k_sb")
@@ -380,12 +380,12 @@ def tile_pgwcrossattention_pa_k_kernel(
                 load_x(r + X_AHEAD)
             if r < PAIRS:
                 add_prior(r)
+            if r + 1 < ROUNDS:
+                sort_words(r + 1)
             if 1 <= r <= ROUNDS:
                 quantise_round(r - 1)
             if r < PAIRS:
                 row_maxima(r)
-            if r + 1 < ROUNDS:
-                sort_words(r + 1)
             if r >= PASS_LAG + 1:
                 finish_v(r - PASS_LAG - 1)
             if 4 <= r < PAIRS + 4:

@@ -48,12 +48,12 @@ def tile_pgwcrossattention_pa_k_kernel(
         ctx.enter_context(tc.manual_schedule())
         keep = ctx.enter_context(tc.tile_pool(name="keep", bufs=1))
         x_pool = ctx.enter_context(tc.tile_pool(name="x", bufs=X_AHEAD + 1))
+        sort_pool = ctx.enter_context(tc.tile_pool(name="sorted", bufs=4))
         stage = ctx.enter_context(tc.tile_pool(name="stage", bufs=3))
-        code_pool = ctx.enter_context(tc.tile_pool(name="codes", bufs=PASS_LAG + 1))
+        code_pool = ctx.enter_context(tc.tile_pool(name="codes", bufs=4))
         batch_pool = ctx.enter_context(tc.tile_pool(name="batch", bufs=B))
-        xt_psum = ctx.enter_context(tc.psum_pool(name="xt_psum", bufs=ROUND_BANKS))
         v_psum = ctx.enter_context(tc.psum_pool(name="v_psum", bufs=2))
-        small_psum = ctx.enter_context(tc.psum_pool(name="small_psum", bufs=2))
+        work_psum = ctx.enter_context(tc.psum_pool(name="work_psum", bufs=6))
 
         ident_bf = keep.tile([P, P], BF16, name="ident_bf")
         make_identity(nc, ident_bf[:])
@@ -78,15 +78,20 @@ def tile_pgwcrossattention_pa_k_kernel(
         nc.vector.memset(rows[:], 0.0)
         ones = keep.tile([P, P], BF16, name="ones")
         nc.vector.memset(ones[:], 1.0)
-        nc.sync.dma_start(out=rows[0:1, H : H + 1], in_=gamma.rearrange("(a n) -> a n", a=1))
-        nc.sync.dma_start(out=rows[0:1, 0:H], in_=bv.rearrange("(a n) -> a n", a=1))
+
+        def load_rows():
+            nc.sync.dma_start(out=rows[0:1, H : H + 1], in_=gamma.rearrange("(a n) -> a n", a=1))
+            nc.sync.dma_start(out=rows[0:1, 0:H], in_=bv.rearrange("(a n) -> a n", a=1))
 
         pi_sb = keep.tile([P, B, BLOCKS, LK], BF16, name="pi_sb")
         k_sb = keep.tile([P, B, BLOCKS, H], BF16, name="k_sb")
-        nc.sync.dma_start(out=k_sb[:], in_=k.rearrange("b (p t) h -> p b t h", t=BLOCKS))
         q_sb = keep.tile([P, B, BLOCKS, H], BF16, name="q_sb")
-        nc.sync.dma_start(out=q_sb[:], in_=q.rearrange("b (p j) h -> p b j h", j=BLOCKS))
-        nc.sync.dma_start(out=pi_sb[:], in_=pi_star.rearrange("b (p j) c -> p b j c", j=BLOCKS))
+
+        def load_softmax_inputs():
+            nc.sync.dma_start(out=k_sb[:], in_=k.rearrange("b (p t) h -> p b t h", t=BLOCKS))
+            nc.sync.dma_start(out=q_sb[:], in_=q.rearrange("b (p j) h -> p b j h", j=BLOCKS))
+            load_rows()
+            nc.sync.dma_start(out=pi_sb[:], in_=pi_star.rearrange("b (p j) c -> p b j c", j=BLOCKS))
 
         w_words = keep.tile([P, GROUPS, H], U32, name="w_words", align_bytes=64)
 
@@ -111,47 +116,54 @@ def tile_pgwcrossattention_pa_k_kernel(
             )
             x_tiles[r] = x_sb
 
+        load_softmax_inputs()
         load_x(0)
-        load_w_scales()
         load_x(1)
+        load_w_scales()
         load_w(0)
         load_x(2)
         load_w(1)
-        for r in range(3, X_AHEAD):
-            load_x(r)
+        load_x(3)
+        load_x(4)
+        load_x(5)
 
-        def transpose_rows(rows_sb, name, factor):
-            flipped = keep.tile([P, B, H_HALVES, LK], BF16, name=name)
-            for b in range(B):
-                bank = xt_psum.tile([P, H_HALVES, BLOCKS, P], BF16, name="qk_bank", tag="xt")
-                for a in range(H_HALVES):
-                    for i in range(BLOCKS):
-                        nc.tensor.transpose(
-                            bank[:, a, i, :], rows_sb[:, b, i, a * P : (a + 1) * P], ident_bf[:]
-                        )
-                nc.vector.tensor_scalar_mul(
-                    out=flipped[:, b], in0=bank[:].rearrange("p a i c -> p a (i c)"), scalar1=factor
-                )
-            return flipped
+        kT = keep.tile([P, B, H_HALVES, LK], BF16, name="kT")
+        qT = keep.tile([P, B, H_HALVES, LQ], BF16, name="qT")
 
-        kT = transpose_rows(k_sb, "kT", 1.0)
-        qT = transpose_rows(q_sb, "qT", 1.0 / SQRT_H)
+        def flip(rows_sb, b):
+            bank = work_psum.tile([P, H_HALVES, BLOCKS, P], BF16, name="qk_bank", tag="work")
+            for a in range(H_HALVES):
+                for i in range(BLOCKS):
+                    nc.tensor.transpose(
+                        bank[:, a, i, :], rows_sb[:, b, i, a * P : (a + 1) * P], ident_bf[:]
+                    )
+            return bank[:].rearrange("p a i c -> p a (i c)")
+
+        def flip_k_and_q(b):
+            nc.scalar.copy(out=kT[:, b], in_=flip(k_sb, b))
+            nc.vector.tensor_scalar_mul(out=qT[:, b], in0=flip(q_sb, b), scalar1=1.0 / SQRT_H)
+
 
         log_pi = keep.tile([P, UNITS, LK], F32, name="log_pi")
-        for b in range(B):
-            units = slice(b * BLOCKS, (b + 1) * BLOCKS)
+        def floors(pair):
+            b, j0 = divmod(2 * pair, BLOCKS)
             nc.vector.tensor_scalar_max(
-                out=log_pi[:, units, :].rearrange("p j (t c) -> p j t c", t=BLOCKS),
-                in0=pi_sb[:, b].rearrange("p j (c t) -> p j t c", t=BLOCKS),
+                out=log_pi[:, 2 * pair : 2 * pair + 2, :].rearrange("p j (t c) -> p j t c", t=BLOCKS),
+                in0=pi_sb[:, b, j0 : j0 + 2].rearrange("p j (c t) -> p j t c", t=BLOCKS),
                 scalar1=FLOOR,
             )
+
+        def logs(pair):
+            units = slice(2 * pair, 2 * pair + 2)
             nc.scalar.activation(out=log_pi[:, units, :], in_=log_pi[:, units, :], func=ACT.Ln)
-        nc.scalar.activation(out=one[:], in_=one[:], func=ACT.Exp)
 
         spread = keep.tile([P, H + 2], F32, name="spread")
-        spread_bank = small_psum.tile([P, H + 2], F32, name="spread_bank", tag="small")
-        nc.tensor.matmul(out=spread_bank[:], lhsT=ones[:], rhs=rows[:], start=True, stop=True)
-        nc.vector.tensor_copy(out=spread[:], in_=spread_bank[:])
+
+        def spread_rows():
+            bank = work_psum.tile([P, H + 2], F32, name="spread_bank", tag="work")
+            nc.tensor.matmul(out=bank[:], lhsT=ones[:], rhs=rows[:], start=True, stop=True)
+            nc.scalar.copy(out=spread[:], in_=bank[:])
+
         bv_f32 = spread[:, 0:H]
         gamma_f32 = spread[:, H : H + 1]
 
@@ -167,38 +179,42 @@ def tile_pgwcrossattention_pa_k_kernel(
             if r < SORT_FROM:
                 word_views[r] = as_loaded
                 return
-            x_sorted = stage.tile([P, ROUND_GROUPS, 2, P], F32, name="x_sorted")
+            x_sorted = sort_pool.tile([P, ROUND_GROUPS, 2, P], F32, name="x_sorted")
             nc.vector.tensor_copy(out=x_sorted[:], in_=as_loaded)
             word_views[r] = x_sorted[:]
 
-        def transpose_round(r):
+        def transpose_round(r, banks=range(ROUND_BANKS)):
             words = word_views[r]
-            grouped = stage.tile([P, ROUND_GROUPS * P * PACK], BF16, name="grouped", align_bytes=64)
-            grouped_words = grouped[:].bitcast(F32).rearrange(
+            if banks[0] == 0:
+                grouped_tiles[r] = stage.tile(
+                    [P, ROUND_GROUPS * P * PACK], BF16, name="grouped", align_bytes=64
+                )
+            grouped_words = grouped_tiles[r][:].bitcast(F32).rearrange(
                 "p (a g c u) -> p a g c u", a=ROUND_BANKS, g=BANK_GROUPS, u=2
             )
-            for a in range(ROUND_BANKS):
-                bank = xt_psum.tile([P, BANK_GROUPS, 2, P], F32, name="xt_bank", tag="xt")
+            for a in banks:
+                bank = work_psum.tile([P, BANK_GROUPS, 2, P], F32, name="xt_bank", tag="work")
                 for g in range(BANK_GROUPS):
                     for u in range(2):
                         nc.tensor.transpose(
                             bank[:, g, u, :], words[:, a * BANK_GROUPS + g, u, :], ident_f32[:]
                         )
-                if r < SORT_FROM and a == ROUND_BANKS - 1:
-                    nc.vector.tensor_copy(
-                        out=grouped_words[:, a], in_=bank[:].rearrange("p g u c -> p g c u")
-                    )
-                else:
-                    nc.scalar.copy(
-                        out=grouped_words[:, a], in_=bank[:].rearrange("p g u c -> p g c u")
-                    )
-            grouped_tiles[r] = grouped
+                nc.scalar.copy(
+                    out=grouped_words[:, a], in_=bank[:].rearrange("p g u c -> p g c u")
+                )
 
-        def quantise_round(r):
+        def quantise_round(r, pieces=1):
             grouped = grouped_tiles[r]
             codes = code_pool.tile([P, ROUND_GROUPS * P], U32, name="codes", align_bytes=64)
             scales = code_pool.tile([P, ROUND_GROUPS * P], U8, name="scales", align_bytes=64)
-            nc.vector.quantize_mx(out=codes[:].bitcast(FP8X4), scales=scales[:], in_=grouped[:])
+            width = ROUND_GROUPS * P // pieces
+            for i in range(pieces):
+                piece = slice(i * width, (i + 1) * width)
+                nc.vector.quantize_mx(
+                    out=codes[:, piece].bitcast(FP8X4),
+                    scales=scales[:, piece],
+                    in_=grouped[:, PACK * i * width : PACK * (i + 1) * width],
+                )
             x_codes[r] = codes
             x_scales[r] = scales
 
@@ -211,11 +227,11 @@ def tile_pgwcrossattention_pa_k_kernel(
             block, part = divmod(r, ROUNDS_PER_BLOCK)
             b, t = divmod(block, BLOCKS)
             if part == 0 and t % 2 == 0:
-                v_banks[b] = v_psum.tile([P, 2, H], F32, name="v_bank")
+                v_banks[b, t // 2] = v_psum.tile([P, 2, H], F32, name="v_bank")
             for i in range(ROUND_GROUPS):
                 g = part * ROUND_GROUPS + i
                 nc.tensor.matmul_mx(
-                    out=v_banks[b][:, t % 2, :],
+                    out=v_banks[b, t // 2][:, t % 2, :],
                     lhsT=x_codes[r][:, i * P : (i + 1) * P].bitcast(FP8X4),
                     lhsT_scale=x_scales[r][:, i * P : (i + 1) * P],
                     rhs=w_words[:, g, :].bitcast(FP8X4),
@@ -234,7 +250,7 @@ def tile_pgwcrossattention_pa_k_kernel(
                 v_grouped[b] = batch_pool.tile([P, H, PACK], BF16, name="v_grouped", align_bytes=64)
             nc.vector.tensor_tensor(
                 out=v_grouped[b][:, :, t0 : t0 + 2],
-                in0=v_banks[b][:].rearrange("p t h -> p h t"),
+                in0=v_banks[b, t // 2][:].rearrange("p t h -> p h t"),
                 in1=bv_f32.unsqueeze(2).to_broadcast([P, H, 2]),
                 op=ALU.add,
             )
@@ -251,8 +267,7 @@ def tile_pgwcrossattention_pa_k_kernel(
         row_sum = keep.tile([P, UNITS], F32, name="row_sum")
         row_scale = keep.tile([P, UNITS], F32, name="row_scale")
         qk_banks = {}
-        z_tiles = {}
-        e_tiles = {}
+        e_bf = keep.tile([P, UNITS, LK], BF16, name="e_bf")
         e_grouped = {}
         e_codes = {}
         e_scales = {}
@@ -260,7 +275,7 @@ def tile_pgwcrossattention_pa_k_kernel(
         def qk_matmuls(pair):
             for unit in (2 * pair, 2 * pair + 1):
                 b, j = divmod(unit, BLOCKS)
-                qk = small_psum.tile([P, LK], F32, name="qk", tag="small")
+                qk = work_psum.tile([P, LK], F32, name="qk", tag="work")
                 for a in range(H_HALVES):
                     nc.tensor.matmul(
                         out=qk[:],
@@ -272,37 +287,33 @@ def tile_pgwcrossattention_pa_k_kernel(
                 qk_banks[unit] = qk
 
         def add_prior(pair):
-            z = stage.tile([P, 2, LK], F32, name="z")
             for i in range(2):
                 nc.vector.scalar_tensor_tensor(
-                    out=z[:, i, :],
+                    out=log_pi[:, 2 * pair + i, :],
                     in0=log_pi[:, 2 * pair + i, :],
                     scalar=gamma_f32,
                     in1=qk_banks[2 * pair + i][:],
                     op0=ALU.mult,
                     op1=ALU.add,
                 )
-            z_tiles[pair] = z
 
         def row_maxima(pair):
             units = slice(2 * pair, 2 * pair + 2)
             nc.vector.reduce_max(
-                out=exp_bias[:, units], in_=z_tiles[pair][:], axis=AXIS.X, negate=True
+                out=exp_bias[:, units], in_=log_pi[:, units, :], axis=AXIS.X, negate=True
             )
 
         def exponentials(pair):
-            e_bf = stage.tile([P, 2, LK], BF16, name="e_bf")
             for i in range(2):
                 unit = 2 * pair + i
                 nc.scalar.activation(
-                    out=e_bf[:, i, :].rearrange("p (u c e) -> p u c e", u=2, e=2),
-                    in_=z_tiles[pair][:, i, :].rearrange("p (u e c) -> p u c e", u=2, e=2),
+                    out=e_bf[:, unit, :].rearrange("p (u c e) -> p u c e", u=2, e=2),
+                    in_=log_pi[:, unit, :].rearrange("p (u e c) -> p u c e", u=2, e=2),
                     func=ACT.Exp,
                     bias=exp_bias[:, unit : unit + 1],
                     scale=1.0,
                     accum_out=row_sum[:, unit : unit + 1],
                 )
-            e_tiles[pair] = e_bf
 
         def transpose_e(pair):
             b, j0 = divmod(2 * pair, BLOCKS)
@@ -310,9 +321,9 @@ def tile_pgwcrossattention_pa_k_kernel(
                 e_grouped[b] = batch_pool.tile(
                     [P, BLOCKS, P, PACK], BF16, name="e_grouped", align_bytes=64
                 )
-            bank = small_psum.tile([P, 2, 2, P], F32, name="eT", tag="small")
+            bank = work_psum.tile([P, 2, 2, P], F32, name="eT", tag="work")
             for i in range(2):
-                words = e_tiles[pair][:, i, :].bitcast(F32)
+                words = e_bf[:, 2 * pair + i, :].bitcast(F32)
                 for u in range(2):
                     nc.tensor.transpose(
                         bank[:, i, u, :], words[:, u * P : (u + 1) * P], ident_f32[:]
@@ -340,7 +351,7 @@ def tile_pgwcrossattention_pa_k_kernel(
         def attend(b):
             o_sb = batch_pool.tile([P, BLOCKS, H], F32, name="o_sb")
             for j0 in range(0, BLOCKS, 2):
-                bank = small_psum.tile([P, 2, H], F32, name="o_bank", tag="small")
+                bank = work_psum.tile([P, 2, H], F32, name="o_bank", tag="work")
                 for i in range(2):
                     j = j0 + i
                     nc.tensor.matmul_mx(
@@ -372,35 +383,65 @@ def tile_pgwcrossattention_pa_k_kernel(
                     out=out[b].rearrange("(p j) h -> p j h", j=BLOCKS)[:, j0 : j0 + 2, :],
                     in_=o_sb[:, j0 : j0 + 2, :],
                 )
-
+        for b in range(B):
+            flip_k_and_q(b)
+        spread_rows()
         qk_matmuls(0)
+        floors(0)
+        floors(1)
+        floors(2)
+        floors(3)
+        logs(0)
+        logs(1)
         sort_words(0)
-        for r in range(ROUNDS + PASS_LAG):
-            if r + X_AHEAD < ROUNDS:
-                load_x(r + X_AHEAD)
-            if r < PAIRS:
-                add_prior(r)
+        transpose_round(0)
+        add_prior(0)
+        row_maxima(0)
+        qk_matmuls(1)
+        logs(2)
+        logs(3)
+        add_prior(1)
+        sort_words(1)
+        transpose_round(1)
+        quantise_round(0)
+        row_maxima(1)
+        qk_matmuls(2)
+        add_prior(2)
+        passes_round(0)
+        qk_matmuls(3)
+        quantise_round(1)
+        add_prior(3)
+        row_maxima(2)
+        exponentials(0)
+        load_x(6)
+        sort_words(2)
+        transpose_round(2)
+        passes_round(1)
+        row_maxima(3)
+        load_x(7)
+        sort_words(3)
+        transpose_round(3)
+        sort_words(4)
+        exponentials(1)
+        quantise_round(2)
+        for r in range(4, ROUNDS + PASS_LAG):
+            if r + 4 < ROUNDS:
+                load_x(r + 4)
             if r + 1 < ROUNDS:
                 sort_words(r + 1)
-            if 1 <= r <= ROUNDS:
-                quantise_round(r - 1)
-            if r < PAIRS:
-                row_maxima(r)
-            if r >= PASS_LAG + 1:
-                finish_v(r - PASS_LAG - 1)
-            if 4 <= r < PAIRS + 4:
-                quantise_e(r - 4)
+            if r <= ROUNDS:
+                quantise_round(r - 1, 2 if r == ROUNDS else 1)
+            finish_v(r - 3)
+            if r in (12, 15):
+                quantise_e(1 if r == 12 else 3)
             if r < ROUNDS:
                 transpose_round(r)
-            if 2 <= r < PAIRS + 2:
-                transpose_e(r - 2)
-            if r >= PASS_LAG:
-                passes_round(r - PASS_LAG)
-            if r + 1 < PAIRS:
-                qk_matmuls(r + 1)
-            if r < PAIRS:
-                exponentials(r)
-            if r == ROUNDS_PER_BATCH + PASS_LAG + 1:
+            passes_round(r - PASS_LAG)
+            if r in (5, 7):
+                exponentials((r - 1) // 2)
+            if r in (8, 10, 12, 14):
+                transpose_e((r - 8) // 2)
+            if r == ROUNDS:
                 attend(0)
         finish_v(ROUNDS - 1)
         attend(1)

@@ -34,8 +34,8 @@ ROUND_FEATURES = ROUND_GROUPS * K_PASS
 BANK_GROUPS = 2
 ROUND_BANKS = ROUND_GROUPS // BANK_GROUPS
 PASS_LAG = 2
-X_AHEAD = 5
-SORT_FROM = 4
+WARM_UP = 24
+UNSORTED = (0, 1, 2, 3, 4)
 
 FLOPS = 2 * B * LK * DIN * H + 2 * B * LQ * LK * H + 2 * B * LQ * LK * H
 
@@ -47,7 +47,7 @@ def tile_pgwcrossattention_pa_k_kernel(
     with ExitStack() as ctx:
         ctx.enter_context(tc.manual_schedule())
         keep = ctx.enter_context(tc.tile_pool(name="keep", bufs=1))
-        x_pool = ctx.enter_context(tc.tile_pool(name="x", bufs=X_AHEAD + 1))
+        x_pool = ctx.enter_context(tc.tile_pool(name="x", bufs=6))
         sort_pool = ctx.enter_context(tc.tile_pool(name="sorted", bufs=4))
         stage = ctx.enter_context(tc.tile_pool(name="stage", bufs=3))
         code_pool = ctx.enter_context(tc.tile_pool(name="codes", bufs=4))
@@ -55,13 +55,14 @@ def tile_pgwcrossattention_pa_k_kernel(
         v_psum = ctx.enter_context(tc.psum_pool(name="v_psum", bufs=2))
         work_psum = ctx.enter_context(tc.psum_pool(name="work_psum", bufs=6))
 
+        ones = keep.tile([P, P], BF16, name="ones")
+        nc.vector.memset(ones[:], 1.0)
         ident_bf = keep.tile([P, P], BF16, name="ident_bf")
         make_identity(nc, ident_bf[:])
         ident_f32 = keep.tile([P, P], F32, name="ident_f32")
         make_identity(nc, ident_f32[:])
 
         w_scales = keep.tile([P, GROUPS, H], U8, name="w_scales", align_bytes=64)
-        nc.vector.memset(w_scales[:].rearrange("p g n -> p (g n)").bitcast(I32), 0)
 
         def load_w_scales():
             for row in range(4):
@@ -76,8 +77,8 @@ def tile_pgwcrossattention_pa_k_kernel(
 
         rows = keep.tile([P, H + 2], BF16, name="rows")
         nc.vector.memset(rows[:], 0.0)
-        ones = keep.tile([P, P], BF16, name="ones")
-        nc.vector.memset(ones[:], 1.0)
+
+        nc.vector.memset(w_scales[:].rearrange("p g n -> p (g n)").bitcast(I32), 0)
 
         def load_rows():
             nc.sync.dma_start(out=rows[0:1, H : H + 1], in_=gamma.rearrange("(a n) -> a n", a=1))
@@ -104,9 +105,13 @@ def tile_pgwcrossattention_pa_k_kernel(
 
         x_tiles = {}
 
-        def load_x(r):
+        def place(r):
             block, part = divmod(r, ROUNDS_PER_BLOCK)
             b, t = divmod(block, BLOCKS)
+            return b, t, part
+
+        def load_x(r):
+            b, t, part = place(r)
             x_sb = x_pool.tile([P, ROUND_FEATURES], BF16, name="x_sb")
             nc.sync.dma_start(
                 out=x_sb[:],
@@ -137,19 +142,26 @@ def tile_pgwcrossattention_pa_k_kernel(
                     nc.tensor.transpose(
                         bank[:, a, i, :], rows_sb[:, b, i, a * P : (a + 1) * P], ident_bf[:]
                     )
-            return bank[:].rearrange("p a i c -> p a (i c)")
+            return bank[:]
 
         def flip_k_and_q(b):
-            nc.scalar.copy(out=kT[:, b], in_=flip(k_sb, b))
-            nc.vector.tensor_scalar_mul(out=qT[:, b], in0=flip(q_sb, b), scalar1=1.0 / SQRT_H)
+            nc.scalar.copy(
+                out=kT[:, b].rearrange("p a (c t) -> p a c t", t=BLOCKS),
+                in_=flip(k_sb, b).rearrange("p a t c -> p a c t"),
+            )
+            nc.vector.tensor_scalar_mul(
+                out=qT[:, b].rearrange("p a (j c) -> p a j c", j=BLOCKS),
+                in0=flip(q_sb, b),
+                scalar1=1.0 / SQRT_H,
+            )
 
 
         log_pi = keep.tile([P, UNITS, LK], F32, name="log_pi")
         def floors(pair):
             b, j0 = divmod(2 * pair, BLOCKS)
             nc.vector.tensor_scalar_max(
-                out=log_pi[:, 2 * pair : 2 * pair + 2, :].rearrange("p j (t c) -> p j t c", t=BLOCKS),
-                in0=pi_sb[:, b, j0 : j0 + 2].rearrange("p j (c t) -> p j t c", t=BLOCKS),
+                out=log_pi[:, 2 * pair : 2 * pair + 2, :],
+                in0=pi_sb[:, b, j0 : j0 + 2],
                 scalar1=FLOOR,
             )
 
@@ -176,92 +188,95 @@ def tile_pgwcrossattention_pa_k_kernel(
             as_loaded = x_tiles[r][:].bitcast(F32).rearrange(
                 "p (g c u) -> p g u c", g=ROUND_GROUPS, u=2
             )
-            if r < SORT_FROM:
-                word_views[r] = as_loaded
-                return
-            x_sorted = sort_pool.tile([P, ROUND_GROUPS, 2, P], F32, name="x_sorted")
-            nc.vector.tensor_copy(out=x_sorted[:], in_=as_loaded)
-            word_views[r] = x_sorted[:]
+            views = [as_loaded[:, g] for g in range(ROUND_GROUPS)]
+            if r not in UNSORTED:
+                x_sorted = sort_pool.tile([P, ROUND_GROUPS, 2, P], F32, name="x_sorted")
+                nc.vector.tensor_copy(out=x_sorted[:], in_=as_loaded)
+                views = [x_sorted[:, g] for g in range(ROUND_GROUPS)]
+            word_views[r] = views
 
-        def transpose_round(r, banks=range(ROUND_BANKS)):
+        def transpose_round(r):
             words = word_views[r]
-            if banks[0] == 0:
-                grouped_tiles[r] = stage.tile(
-                    [P, ROUND_GROUPS * P * PACK], BF16, name="grouped", align_bytes=64
-                )
+            grouped_tiles[r] = stage.tile(
+                [P, ROUND_GROUPS * P * PACK], BF16, name="grouped", align_bytes=64
+            )
             grouped_words = grouped_tiles[r][:].bitcast(F32).rearrange(
                 "p (a g c u) -> p a g c u", a=ROUND_BANKS, g=BANK_GROUPS, u=2
             )
-            for a in banks:
+            for a in range(ROUND_BANKS):
                 bank = work_psum.tile([P, BANK_GROUPS, 2, P], F32, name="xt_bank", tag="work")
                 for g in range(BANK_GROUPS):
                     for u in range(2):
                         nc.tensor.transpose(
-                            bank[:, g, u, :], words[:, a * BANK_GROUPS + g, u, :], ident_f32[:]
+                            bank[:, g, u, :], words[a * BANK_GROUPS + g][:, u, :], ident_f32[:]
                         )
                 nc.scalar.copy(
                     out=grouped_words[:, a], in_=bank[:].rearrange("p g u c -> p g c u")
                 )
 
-        def quantise_round(r, pieces=1):
-            grouped = grouped_tiles[r]
-            codes = code_pool.tile([P, ROUND_GROUPS * P], U32, name="codes", align_bytes=64)
-            scales = code_pool.tile([P, ROUND_GROUPS * P], U8, name="scales", align_bytes=64)
-            width = ROUND_GROUPS * P // pieces
-            for i in range(pieces):
-                piece = slice(i * width, (i + 1) * width)
-                nc.vector.quantize_mx(
-                    out=codes[:, piece].bitcast(FP8X4),
-                    scales=scales[:, piece],
-                    in_=grouped[:, PACK * i * width : PACK * (i + 1) * width],
-                )
-            x_codes[r] = codes
-            x_scales[r] = scales
+        def quantise_round(r, first=0, last=ROUND_GROUPS):
+            if first == 0:
+                x_codes[r] = code_pool.tile([P, ROUND_GROUPS * P], U32, name="codes", align_bytes=64)
+                x_scales[r] = code_pool.tile([P, ROUND_GROUPS * P], U8, name="scales", align_bytes=64)
+            piece = slice(first * P, last * P)
+            nc.vector.quantize_mx(
+                out=x_codes[r][:, piece].bitcast(FP8X4),
+                scales=x_scales[r][:, piece],
+                in_=grouped_tiles[r][:, first * P * PACK : last * P * PACK],
+            )
 
         v_banks = {}
         v_grouped = {}
         v_codes = {}
         v_scales = {}
 
-        def passes_round(r):
-            block, part = divmod(r, ROUNDS_PER_BLOCK)
-            b, t = divmod(block, BLOCKS)
-            if part == 0 and t % 2 == 0:
+        def passes_round(r, cols=slice(0, H), out_bank=None):
+            b, t, part = place(r)
+            if part == 0 and t % 2 == 0 and cols.start == 0:
                 v_banks[b, t // 2] = v_psum.tile([P, 2, H], F32, name="v_bank")
             for i in range(ROUND_GROUPS):
                 g = part * ROUND_GROUPS + i
                 nc.tensor.matmul_mx(
-                    out=v_banks[b, t // 2][:, t % 2, :],
+                    out=v_banks[b, t // 2][:, t % 2, cols] if out_bank is None else out_bank[:],
                     lhsT=x_codes[r][:, i * P : (i + 1) * P].bitcast(FP8X4),
                     lhsT_scale=x_scales[r][:, i * P : (i + 1) * P],
-                    rhs=w_words[:, g, :].bitcast(FP8X4),
-                    rhs_scale=w_scales[:, g, :],
+                    rhs=w_words[:, g, cols].bitcast(FP8X4),
+                    rhs_scale=w_scales[:, g, cols],
                     start=(g == 0),
                     stop=(g == GROUPS - 1),
                 )
 
-        def finish_v(r):
-            block, part = divmod(r, ROUNDS_PER_BLOCK)
-            b, t = divmod(block, BLOCKS)
-            if part != ROUNDS_PER_BLOCK - 1 or t % 2 == 0:
-                return
-            t0 = t - 1
-            if t0 == 0:
-                v_grouped[b] = batch_pool.tile([P, H, PACK], BF16, name="v_grouped", align_bytes=64)
+        v_rows = {}
+        o_tiles = {}
+
+        def finish_blocks(b, t0, count, cols=slice(0, H), bank=None):
+            if b not in v_rows:
+                v_rows[b] = batch_pool.tile([P, BLOCKS, H], BF16, name="v_rows")
             nc.vector.tensor_tensor(
-                out=v_grouped[b][:, :, t0 : t0 + 2],
-                in0=v_banks[b, t // 2][:].rearrange("p t h -> p h t"),
-                in1=bv_f32.unsqueeze(2).to_broadcast([P, H, 2]),
+                out=v_rows[b][:, t0 : t0 + count, cols],
+                in0=v_banks[b, t0 // 2][:, t0 % 2 : t0 % 2 + count, cols]
+                if bank is None
+                else bank[:].unsqueeze(1),
+                in1=bv_f32[:, cols].unsqueeze(1).to_broadcast([P, count, cols.stop - cols.start]),
                 op=ALU.add,
             )
-            if t0 + 2 == BLOCKS:
+
+        def group_v(b, cols=slice(0, H)):
+            if b not in v_grouped:
+                v_grouped[b] = batch_pool.tile([P, H, PACK], BF16, name="v_grouped", align_bytes=64)
+            nc.vector.tensor_copy(
+                out=v_grouped[b][:, cols], in_=v_rows[b][:, :, cols].rearrange("p t h -> p h t")
+            )
+
+        def quantise_v(b, cols=slice(0, H)):
+            if b not in v_codes:
                 v_codes[b] = batch_pool.tile([P, H], U32, name="v_codes", align_bytes=64)
                 v_scales[b] = batch_pool.tile([P, H], U8, name="v_scales", align_bytes=64)
-                nc.vector.quantize_mx(
-                    out=v_codes[b][:].bitcast(FP8X4),
-                    scales=v_scales[b][:],
-                    in_=v_grouped[b][:].rearrange("p h t -> p (h t)"),
-                )
+            nc.vector.quantize_mx(
+                out=v_codes[b][:, cols].bitcast(FP8X4),
+                scales=v_scales[b][:, cols],
+                in_=v_grouped[b][:, cols].rearrange("p h t -> p (h t)"),
+            )
 
         exp_bias = keep.tile([P, UNITS], F32, name="exp_bias")
         row_sum = keep.tile([P, UNITS], F32, name="row_sum")
@@ -303,17 +318,19 @@ def tile_pgwcrossattention_pa_k_kernel(
                 out=exp_bias[:, units], in_=log_pi[:, units, :], axis=AXIS.X, negate=True
             )
 
+        def exponential(unit):
+            nc.scalar.activation(
+                out=e_bf[:, unit, :].rearrange("p (u c e) -> p u c e", u=2, e=2),
+                in_=log_pi[:, unit, :].rearrange("p (c u e) -> p u c e", u=2, e=2),
+                func=ACT.Exp,
+                bias=exp_bias[:, unit : unit + 1],
+                scale=1.0,
+                accum_out=row_sum[:, unit : unit + 1],
+            )
+
         def exponentials(pair):
-            for i in range(2):
-                unit = 2 * pair + i
-                nc.scalar.activation(
-                    out=e_bf[:, unit, :].rearrange("p (u c e) -> p u c e", u=2, e=2),
-                    in_=log_pi[:, unit, :].rearrange("p (u e c) -> p u c e", u=2, e=2),
-                    func=ACT.Exp,
-                    bias=exp_bias[:, unit : unit + 1],
-                    scale=1.0,
-                    accum_out=row_sum[:, unit : unit + 1],
-                )
+            exponential(2 * pair)
+            exponential(2 * pair + 1)
 
         def transpose_e(pair):
             b, j0 = divmod(2 * pair, BLOCKS)
@@ -347,6 +364,41 @@ def tile_pgwcrossattention_pa_k_kernel(
             )
             units = slice(b * BLOCKS, (b + 1) * BLOCKS)
             nc.vector.reciprocal(out=row_scale[:, units], in_=row_sum[:, units])
+
+        def attend_half(b, cols, on_vector):
+            if b not in o_tiles:
+                o_tiles[b] = batch_pool.tile([P, BLOCKS, H], F32, name="o_sb")
+            bank = work_psum.tile([P, BLOCKS, P], F32, name="o_half", tag="work")
+            for j in range(BLOCKS):
+                nc.tensor.matmul_mx(
+                    out=bank[:, j, :],
+                    lhsT=e_codes[b][:, j * P : (j + 1) * P].bitcast(FP8X4),
+                    lhsT_scale=e_scales[b][:, j * P : (j + 1) * P],
+                    rhs=v_codes[b][:, cols].bitcast(FP8X4),
+                    rhs_scale=v_scales[b][:, cols],
+                    start=True,
+                    stop=True,
+                )
+            units = slice(b * BLOCKS, (b + 1) * BLOCKS)
+            if on_vector:
+                nc.vector.tensor_tensor(
+                    out=o_tiles[b][:, :, cols],
+                    in0=bank[:],
+                    in1=row_scale[:, units].unsqueeze(2).to_broadcast([P, BLOCKS, P]),
+                    op=ALU.mult,
+                )
+            else:
+                for j in range(BLOCKS):
+                    nc.scalar.activation(
+                        out=o_tiles[b][:, j, cols],
+                        in_=bank[:, j, :],
+                        func=ACT.Copy,
+                        scale=row_scale[:, b * BLOCKS + j : b * BLOCKS + j + 1],
+                    )
+            nc.sync.dma_start(
+                out=out[b].rearrange("(p j) h -> p j h", j=BLOCKS)[:, :, cols],
+                in_=o_tiles[b][:, :, cols],
+            )
 
         def attend(b):
             o_sb = batch_pool.tile([P, BLOCKS, H], F32, name="o_sb")
@@ -383,6 +435,9 @@ def tile_pgwcrossattention_pa_k_kernel(
                     out=out[b].rearrange("(p j) h -> p j h", j=BLOCKS)[:, j0 : j0 + 2, :],
                     in_=o_sb[:, j0 : j0 + 2, :],
                 )
+        warm_bank = work_psum.tile([P, P], F32, name="warm_bank", tag="work")
+        for i in range(WARM_UP):
+            nc.tensor.matmul(out=warm_bank[:], lhsT=ones[:], rhs=ones[:], start=True, stop=True)
         for b in range(B):
             flip_k_and_q(b)
         spread_rows()
@@ -424,24 +479,60 @@ def tile_pgwcrossattention_pa_k_kernel(
         sort_words(4)
         exponentials(1)
         quantise_round(2)
-        for r in range(4, ROUNDS + PASS_LAG):
-            if r + 4 < ROUNDS:
-                load_x(r + 4)
-            if r + 1 < ROUNDS:
-                sort_words(r + 1)
-            if r <= ROUNDS:
-                quantise_round(r - 1, 2 if r == ROUNDS else 1)
-            finish_v(r - 3)
-            if r in (12, 15):
-                quantise_e(1 if r == 12 else 3)
-            if r < ROUNDS:
-                transpose_round(r)
+        for r in (4, 5):
+            load_x(r + 4)
+            sort_words(r + 1)
+            quantise_round(r - 1)
+            transpose_round(r)
             passes_round(r - PASS_LAG)
-            if r in (5, 7):
-                exponentials((r - 1) // 2)
-            if r in (8, 10, 12, 14):
-                transpose_e((r - 8) // 2)
-            if r == ROUNDS:
-                attend(0)
-        finish_v(ROUNDS - 1)
-        attend(1)
+        sort_words(7)
+        quantise_round(5)
+        for c0 in range(6, ROUNDS, 2):
+            c1 = c0 + 1
+            for r in (c0 + 4, c1 + 4):
+                if r < ROUNDS:
+                    load_x(r)
+            if c0 == 8:
+                finish_blocks(0, 0, 2)
+            if c0 == 12:
+                finish_blocks(0, 2, 2)
+                group_v(0)
+                quantise_v(0)
+            if c0 == 14:
+                finish_blocks(1, 0, 2)
+            transpose_round(c0)
+            transpose_round(c1)
+            if c0 >= 8:
+                transpose_e((c0 - 8) // 2)
+            if c0 <= 12:
+                exponential(c0 // 2 + 1)
+            passes_round(c0 - PASS_LAG)
+            passes_round(c1 - PASS_LAG)
+            if c0 + 2 < ROUNDS:
+                sort_words(c0 + 2)
+            quantise_round(c0)
+            if c1 + 2 < ROUNDS:
+                sort_words(c1 + 2)
+            if c1 < ROUNDS - 1:
+                quantise_round(c1)
+            if c0 == 12:
+                quantise_e(1)
+        quantise_round(ROUNDS - 1, 0, ROUND_GROUPS // 2)
+        finish_blocks(1, 2, 1)
+        quantise_round(ROUNDS - 1, ROUND_GROUPS // 2, ROUND_GROUPS)
+        quantise_e(3)
+        attend(0)
+        low, high = slice(0, P), slice(P, H)
+        passes_round(ROUNDS - 2, low)
+        passes_round(ROUNDS - 1, low)
+        high_bank = work_psum.tile([P, P], F32, name="high_bank", tag="work")
+        passes_round(ROUNDS - 2, high, high_bank)
+        passes_round(ROUNDS - 1, high, high_bank)
+        finish_blocks(1, 3, 1, low)
+        group_v(1, low)
+        quantise_v(1, low)
+        attend_half(1, low, False)
+        finish_blocks(1, 3, 1, high, high_bank)
+        group_v(1, high)
+        quantise_v(1, high)
+        attend_half(1, high, True)

@@ -479,44 +479,26 @@ def tile_pgwcrossattention_pa_k_kernel(
         sort_words(4)
         exponentials(1)
         quantise_round(2)
-        for r in (4, 5):
-            load_x(r + 4)
-            sort_words(r + 1)
+        for r in range(4, ROUNDS):
+            if r + 4 < ROUNDS:
+                load_x(r + 4)
+            if r + 1 < ROUNDS:
+                sort_words(r + 1)
             quantise_round(r - 1)
+            if r in (6, 10, 14):
+                finish_blocks((r - 6) // 8, (r - 6) // 2 % 4, 2)
+            if r == 11:
+                group_v(0)
+            if r == 12:
+                quantise_v(0)
+            if r == 13:
+                quantise_e(1)
             transpose_round(r)
             passes_round(r - PASS_LAG)
-        sort_words(7)
-        quantise_round(5)
-        for c0 in range(6, ROUNDS, 2):
-            c1 = c0 + 1
-            for r in (c0 + 4, c1 + 4):
-                if r < ROUNDS:
-                    load_x(r)
-            if c0 == 8:
-                finish_blocks(0, 0, 2)
-            if c0 == 12:
-                finish_blocks(0, 2, 2)
-                group_v(0)
-                quantise_v(0)
-            if c0 == 14:
-                finish_blocks(1, 0, 2)
-            transpose_round(c0)
-            transpose_round(c1)
-            if c0 >= 8:
-                transpose_e((c0 - 8) // 2)
-            if c0 <= 12:
-                exponential(c0 // 2 + 1)
-            passes_round(c0 - PASS_LAG)
-            passes_round(c1 - PASS_LAG)
-            if c0 + 2 < ROUNDS:
-                sort_words(c0 + 2)
-            quantise_round(c0)
-            if c1 + 2 < ROUNDS:
-                sort_words(c1 + 2)
-            if c1 < ROUNDS - 1:
-                quantise_round(c1)
-            if c0 == 12:
-                quantise_e(1)
+            if r in (5, 7, 9, 11):
+                exponential((r + 3) // 2)
+            if r in (8, 10, 12, 14):
+                transpose_e((r - 8) // 2)
         quantise_round(ROUNDS - 1, 0, ROUND_GROUPS // 2)
         finish_blocks(1, 2, 1)
         quantise_round(ROUNDS - 1, ROUND_GROUPS // 2, ROUND_GROUPS)

@@ -195,15 +195,16 @@ def tile_pgwcrossattention_pa_k_kernel(
                 views = [x_sorted[:, g] for g in range(ROUND_GROUPS)]
             word_views[r] = views
 
-        def transpose_round(r):
+        def transpose_round(r, banks=range(ROUND_BANKS)):
             words = word_views[r]
-            grouped_tiles[r] = stage.tile(
-                [P, ROUND_GROUPS * P * PACK], BF16, name="grouped", align_bytes=64
-            )
+            if banks[0] == 0:
+                grouped_tiles[r] = stage.tile(
+                    [P, ROUND_GROUPS * P * PACK], BF16, name="grouped", align_bytes=64
+                )
             grouped_words = grouped_tiles[r][:].bitcast(F32).rearrange(
                 "p (a g c u) -> p a g c u", a=ROUND_BANKS, g=BANK_GROUPS, u=2
             )
-            for a in range(ROUND_BANKS):
+            for a in banks:
                 bank = work_psum.tile([P, BANK_GROUPS, 2, P], F32, name="xt_bank", tag="work")
                 for g in range(BANK_GROUPS):
                     for u in range(2):
@@ -230,11 +231,11 @@ def tile_pgwcrossattention_pa_k_kernel(
         v_codes = {}
         v_scales = {}
 
-        def passes_round(r, cols=slice(0, H), out_bank=None):
+        def passes_round(r, cols=slice(0, H), out_bank=None, groups=range(ROUND_GROUPS)):
             b, t, part = place(r)
-            if part == 0 and t % 2 == 0 and cols.start == 0:
+            if part == 0 and t % 2 == 0 and cols.start == 0 and groups[0] == 0:
                 v_banks[b, t // 2] = v_psum.tile([P, 2, H], F32, name="v_bank")
-            for i in range(ROUND_GROUPS):
+            for i in groups:
                 g = part * ROUND_GROUPS + i
                 nc.tensor.matmul_mx(
                     out=v_banks[b, t // 2][:, t % 2, cols] if out_bank is None else out_bank[:],
@@ -493,8 +494,12 @@ def tile_pgwcrossattention_pa_k_kernel(
                 quantise_v(0)
             if r == 13:
                 quantise_e(1)
-            transpose_round(r)
-            passes_round(r - PASS_LAG)
+            for half in range(2):
+                transpose_round(r, range(half * ROUND_BANKS // 2, (half + 1) * ROUND_BANKS // 2))
+                passes_round(
+                    r - PASS_LAG,
+                    groups=range(half * ROUND_GROUPS // 2, (half + 1) * ROUND_GROUPS // 2),
+                )
             if r in (5, 7, 9, 11):
                 exponential((r + 3) // 2)
             if r in (8, 10, 12, 14):

from contextlib import ExitStack

import concourse.mybir as mybir
from concourse.masks import make_identity

F32 = mybir.dt.float32
BF16 = mybir.dt.bfloat16
I32 = mybir.dt.int32
U32 = mybir.dt.uint32
U8 = mybir.dt.uint8
FP8X4 = mybir.dt.float8_e4m3fn_x4
ALU = mybir.AluOpType
ACT = mybir.ActivationFunctionType
AXIS = mybir.AxisListType

B, LQ, LK, DIN, H = 2, 512, 512, 8192, 256
FLOOR = 1e-9
SQRT_H = 16.0

P = 128
PACK = 4
K_PASS = P * PACK
GROUPS = DIN // K_PASS
BLOCKS = LK // P
UNITS = B * BLOCKS
PAIRS = UNITS // 2
H_HALVES = H // P

ROUND_GROUPS = 8
ROUNDS_PER_BLOCK = GROUPS // ROUND_GROUPS
ROUNDS = B * BLOCKS * ROUNDS_PER_BLOCK
ROUNDS_PER_BATCH = ROUNDS // B
ROUND_FEATURES = ROUND_GROUPS * K_PASS
BANK_GROUPS = 2
ROUND_BANKS = ROUND_GROUPS // BANK_GROUPS
PASS_LAG = 2
WARM_UP = 24
UNSORTED = (0, 1, 2, 3, 4)

FLOPS = 2 * B * LK * DIN * H + 2 * B * LQ * LK * H + 2 * B * LQ * LK * H


def tile_pgwcrossattention_pa_k_kernel(
    tc, q, k, v_ret, pi_star, Wv_words, Wv_scales, bv, gamma, out
):
    nc = tc.nc
    with ExitStack() as ctx:
        ctx.enter_context(tc.manual_schedule())
        keep = ctx.enter_context(tc.tile_pool(name="keep", bufs=1))
        x_pool = ctx.enter_context(tc.tile_pool(name="x", bufs=6))
        sort_pool = ctx.enter_context(tc.tile_pool(name="sorted", bufs=4))
        stage = ctx.enter_context(tc.tile_pool(name="stage", bufs=3))
        code_pool = ctx.enter_context(tc.tile_pool(name="codes", bufs=4))
        batch_pool = ctx.enter_context(tc.tile_pool(name="batch", bufs=B))
        v_psum = ctx.enter_context(tc.psum_pool(name="v_psum", bufs=2))
        work_psum = ctx.enter_context(tc.psum_pool(name="work_psum", bufs=6))

        ones = keep.tile([P, P], BF16, name="ones")
        nc.vector.memset(ones[:], 1.0)
        ident_bf = keep.tile([P, P], BF16, name="ident_bf")
        make_identity(nc, ident_bf[:])
        ident_f32 = keep.tile([P, P], F32, name="ident_f32")
        make_identity(nc, ident_f32[:])

        w_scales = keep.tile([P, GROUPS, H], U8, name="w_scales", align_bytes=64)

        def load_w_scales():
            for row in range(4):
                nc.sync.dma_start(
                    out=w_scales[row:P:32].bitcast(I32),
                    in_=Wv_scales[:, row:16:4, :].rearrange("g s n -> s g n").bitcast(I32),
                )

        one = keep.tile([P, 1], F32, name="one")
        nc.vector.memset(one[:], 1.0)
        nc.scalar.activation(out=one[:], in_=one[:], func=ACT.Ln)

        rows = keep.tile([P, H + 2], BF16, name="rows")
        nc.vector.memset(rows[:], 0.0)

        nc.vector.memset(w_scales[:].rearrange("p g n -> p (g n)").bitcast(I32), 0)

        def load_rows():
            nc.sync.dma_start(out=rows[0:1, H : H + 1], in_=gamma.rearrange("(a n) -> a n", a=1))
            nc.sync.dma_start(out=rows[0:1, 0:H], in_=bv.rearrange("(a n) -> a n", a=1))

        pi_sb = keep.tile([P, B, BLOCKS, LK], BF16, name="pi_sb")
        k_sb = keep.tile([P, B, BLOCKS, H], BF16, name="k_sb")
        q_sb = keep.tile([P, B, BLOCKS, H], BF16, name="q_sb")

        def load_softmax_inputs():
            nc.sync.dma_start(out=k_sb[:], in_=k.rearrange("b (p t) h -> p b t h", t=BLOCKS))
            nc.sync.dma_start(out=q_sb[:], in_=q.rearrange("b (p j) h -> p b j h", j=BLOCKS))
            load_rows()
            nc.sync.dma_start(out=pi_sb[:], in_=pi_star.rearrange("b (p j) c -> p b j c", j=BLOCKS))

        w_words = keep.tile([P, GROUPS, H], U32, name="w_words", align_bytes=64)

        def load_w(part):
            groups = slice(part * ROUND_GROUPS, (part + 1) * ROUND_GROUPS)
            nc.sync.dma_start(
                out=w_words[:, groups, :].bitcast(I32),
                in_=Wv_words[groups].rearrange("g p n t -> p g (n t)").bitcast(I32),
            )

        x_tiles = {}

        def place(r):
            block, part = divmod(r, ROUNDS_PER_BLOCK)
            b, t = divmod(block, BLOCKS)
            return b, t, part

        def load_x(r):
            b, t, part = place(r)
            x_sb = x_pool.tile([P, ROUND_FEATURES], BF16, name="x_sb")
            nc.sync.dma_start(
                out=x_sb[:],
                in_=v_ret[b].rearrange("(p t) f -> p t f", t=BLOCKS)[
                    :, t, part * ROUND_FEATURES : (part + 1) * ROUND_FEATURES
                ],
            )
            x_tiles[r] = x_sb

        load_softmax_inputs()
        load_x(0)
        load_x(1)
        load_w_scales()
        load_w(0)
        load_x(2)
        load_w(1)
        load_x(3)
        load_x(4)
        load_x(5)

        kT = keep.tile([P, B, H_HALVES, LK], BF16, name="kT")
        qT = keep.tile([P, B, H_HALVES, LQ], BF16, name="qT")

        def flip(rows_sb, b):
            bank = work_psum.tile([P, H_HALVES, BLOCKS, P], BF16, name="qk_bank", tag="work")
            for a in range(H_HALVES):
                for i in range(BLOCKS):
                    nc.tensor.transpose(
                        bank[:, a, i, :], rows_sb[:, b, i, a * P : (a + 1) * P], ident_bf[:]
                    )
            return bank[:]

        def flip_k_and_q(b):
            nc.scalar.copy(
                out=kT[:, b].rearrange("p a (c t) -> p a c t", t=BLOCKS),
                in_=flip(k_sb, b).rearrange("p a t c -> p a c t"),
            )
            nc.vector.tensor_scalar_mul(
                out=qT[:, b].rearrange("p a (j c) -> p a j c", j=BLOCKS),
                in0=flip(q_sb, b),
                scalar1=1.0 / SQRT_H,
            )


        log_pi = keep.tile([P, UNITS, LK], F32, name="log_pi")
        def floors(pair):
            b, j0 = divmod(2 * pair, BLOCKS)
            nc.vector.tensor_scalar_max(
                out=log_pi[:, 2 * pair : 2 * pair + 2, :],
                in0=pi_sb[:, b, j0 : j0 + 2],
                scalar1=FLOOR,
            )

        def logs(pair):
            units = slice(2 * pair, 2 * pair + 2)
            nc.scalar.activation(out=log_pi[:, units, :], in_=log_pi[:, units, :], func=ACT.Ln)

        spread = keep.tile([P, H + 2], F32, name="spread")

        def spread_rows():
            bank = work_psum.tile([P, H + 2], F32, name="spread_bank", tag="work")
            nc.tensor.matmul(out=bank[:], lhsT=ones[:], rhs=rows[:], start=True, stop=True)
            nc.scalar.copy(out=spread[:], in_=bank[:])

        bv_f32 = spread[:, 0:H]
        gamma_f32 = spread[:, H : H + 1]

        word_views = {}
        grouped_tiles = {}
        x_codes = {}
        x_scales = {}

        def sort_words(r):
            as_loaded = x_tiles[r][:].bitcast(F32).rearrange(
                "p (g c u) -> p g u c", g=ROUND_GROUPS, u=2
            )
            views = [as_loaded[:, g] for g in range(ROUND_GROUPS)]
            if r not in UNSORTED:
                x_sorted = sort_pool.tile([P, ROUND_GROUPS, 2, P], F32, name="x_sorted")
                nc.vector.tensor_copy(out=x_sorted[:], in_=as_loaded)
                views = [x_sorted[:, g] for g in range(ROUND_GROUPS)]
            word_views[r] = views

        def transpose_round(r, banks=range(ROUND_BANKS)):
            words = word_views[r]
            if banks[0] == 0:
                grouped_tiles[r] = stage.tile(
                    [P, ROUND_GROUPS * P * PACK], BF16, name="grouped", align_bytes=64
                )
            grouped_words = grouped_tiles[r][:].bitcast(F32).rearrange(
                "p (a g c u) -> p a g c u", a=ROUND_BANKS, g=BANK_GROUPS, u=2
            )
            for a in banks:
                bank = work_psum.tile([P, BANK_GROUPS, 2, P], F32, name="xt_bank", tag="work")
                for g in range(BANK_GROUPS):
                    for u in range(2):
                        nc.tensor.transpose(
                            bank[:, g, u, :], words[a * BANK_GROUPS + g][:, u, :], ident_f32[:]
                        )
                nc.scalar.copy(
                    out=grouped_words[:, a], in_=bank[:].rearrange("p g u c -> p g c u")
                )

        def quantise_round(r, first=0, last=ROUND_GROUPS):
            if first == 0:
                x_codes[r] = code_pool.tile([P, ROUND_GROUPS * P], U32, name="codes", align_bytes=64)
                x_scales[r] = code_pool.tile([P, ROUND_GROUPS * P], U8, name="scales", align_bytes=64)
            piece = slice(first * P, last * P)
            nc.vector.quantize_mx(
                out=x_codes[r][:, piece].bitcast(FP8X4),
                scales=x_scales[r][:, piece],
                in_=grouped_tiles[r][:, first * P * PACK : last * P * PACK],
            )

        v_banks = {}
        v_grouped = {}
        v_codes = {}
        v_scales = {}

        def passes_round(r, cols=slice(0, H), out_bank=None, groups=range(ROUND_GROUPS)):
            b, t, part = place(r)
            if part == 0 and t % 2 == 0 and cols.start == 0 and groups[0] == 0:
                v_banks[b, t // 2] = v_psum.tile([P, 2, H], F32, name="v_bank")
            for i in groups:
                g = part * ROUND_GROUPS + i
                nc.tensor.matmul_mx(
                    out=v_banks[b, t // 2][:, t % 2, cols] if out_bank is None else out_bank[:],
                    lhsT=x_codes[r][:, i * P : (i + 1) * P].bitcast(FP8X4),
                    lhsT_scale=x_scales[r][:, i * P : (i + 1) * P],
                    rhs=w_words[:, g, cols].bitcast(FP8X4),
                    rhs_scale=w_scales[:, g, cols],
                    start=(g == 0),
                    stop=(g == GROUPS - 1),
                )

        v_rows = {}
        o_tiles = {}

        def finish_blocks(b, t0, count, cols=slice(0, H), bank=None):
            if b not in v_rows:
                v_rows[b] = batch_pool.tile([P, BLOCKS, H], BF16, name="v_rows")
            nc.vector.tensor_tensor(
                out=v_rows[b][:, t0 : t0 + count, cols],
                in0=v_banks[b, t0 // 2][:, t0 % 2 : t0 % 2 + count, cols]
                if bank is None
                else bank[:].unsqueeze(1),
                in1=bv_f32[:, cols].unsqueeze(1).to_broadcast([P, count, cols.stop - cols.start]),
                op=ALU.add,
            )

        def group_v(b, cols=slice(0, H)):
            if b not in v_grouped:
                v_grouped[b] = batch_pool.tile([P, H, PACK], BF16, name="v_grouped", align_bytes=64)
            nc.vector.tensor_copy(
                out=v_grouped[b][:, cols], in_=v_rows[b][:, :, cols].rearrange("p t h -> p h t")
            )

        def quantise_v(b, cols=slice(0, H)):
            if b not in v_codes:
                v_codes[b] = batch_pool.tile([P, H], U32, name="v_codes", align_bytes=64)
                v_scales[b] = batch_pool.tile([P, H], U8, name="v_scales", align_bytes=64)
            nc.vector.quantize_mx(
                out=v_codes[b][:, cols].bitcast(FP8X4),
                scales=v_scales[b][:, cols],
                in_=v_grouped[b][:, cols].rearrange("p h t -> p (h t)"),
            )

        exp_bias = keep.tile([P, UNITS], F32, name="exp_bias")
        row_sum = keep.tile([P, UNITS], F32, name="row_sum")
        row_scale = keep.tile([P, UNITS], F32, name="row_scale")
        qk_banks = {}
        e_bf = keep.tile([P, UNITS, LK], BF16, name="e_bf")
        e_grouped = {}
        e_codes = {}
        e_scales = {}

        def qk_matmuls(pair):
            for unit in (2 * pair, 2 * pair + 1):
                b, j = divmod(unit, BLOCKS)
                qk = work_psum.tile([P, LK], F32, name="qk", tag="work")
                for a in range(H_HALVES):
                    nc.tensor.matmul(
                        out=qk[:],
                        lhsT=qT[:, b, a, j * P : (j + 1) * P],
                        rhs=kT[:, b, a, :],
                        start=(a == 0),
                        stop=(a == H_HALVES - 1),
                    )
                qk_banks[unit] = qk

        def add_prior(pair):
            for i in range(2):
                nc.vector.scalar_tensor_tensor(
                    out=log_pi[:, 2 * pair + i, :],
                    in0=log_pi[:, 2 * pair + i, :],
                    scalar=gamma_f32,
                    in1=qk_banks[2 * pair + i][:],
                    op0=ALU.mult,
                    op1=ALU.add,
                )

        def row_maxima(pair):
            units = slice(2 * pair, 2 * pair + 2)
            nc.vector.reduce_max(
                out=exp_bias[:, units], in_=log_pi[:, units, :], axis=AXIS.X, negate=True
            )

        def exponential(unit):
            nc.scalar.activation(
                out=e_bf[:, unit, :].rearrange("p (u c e) -> p u c e", u=2, e=2),
                in_=log_pi[:, unit, :].rearrange("p (c u e) -> p u c e", u=2, e=2),
                func=ACT.Exp,
                bias=exp_bias[:, unit : unit + 1],
                scale=1.0,
                accum_out=row_sum[:, unit : unit + 1],
            )

        def exponentials(pair):
            exponential(2 * pair)
            exponential(2 * pair + 1)

        def transpose_e(pair):
            b, j0 = divmod(2 * pair, BLOCKS)
            if j0 == 0:
                e_grouped[b] = batch_pool.tile(
                    [P, BLOCKS, P, PACK], BF16, name="e_grouped", align_bytes=64
                )
            bank = work_psum.tile([P, 2, 2, P], F32, name="eT", tag="work")
            for i in range(2):
                words = e_bf[:, 2 * pair + i, :].bitcast(F32)
                for u in range(2):
                    nc.tensor.transpose(
                        bank[:, i, u, :], words[:, u * P : (u + 1) * P], ident_f32[:]
                    )
            nc.scalar.copy(
                out=e_grouped[b][:].rearrange("p j c t -> p j (c t)").bitcast(F32)
                .rearrange("p j (c u) -> p j c u", u=2)[:, j0 : j0 + 2],
                in_=bank[:].rearrange("p i u c -> p i c u"),
            )

        def quantise_e(pair):
            b, j0 = divmod(2 * pair, BLOCKS)
            if j0 + 2 != BLOCKS:
                return
            e_codes[b] = batch_pool.tile([P, LQ], U32, name="e_codes", align_bytes=64)
            e_scales[b] = batch_pool.tile([P, LQ], U8, name="e_scales", align_bytes=64)
            nc.vector.quantize_mx(
                out=e_codes[b][:].bitcast(FP8X4),
                scales=e_scales[b][:],
                in_=e_grouped[b][:].rearrange("p j c t -> p (j c t)"),
            )
            units = slice(b * BLOCKS, (b + 1) * BLOCKS)
            nc.vector.reciprocal(out=row_scale[:, units], in_=row_sum[:, units])

        def attend_half(b, cols, on_vector):
            if b not in o_tiles:
                o_tiles[b] = batch_pool.tile([P, BLOCKS, H], F32, name="o_sb")
            bank = work_psum.tile([P, BLOCKS, P], F32, name="o_half", tag="work")
            for j in range(BLOCKS):
                nc.tensor.matmul_mx(
                    out=bank[:, j, :],
                    lhsT=e_codes[b][:, j * P : (j + 1) * P].bitcast(FP8X4),
                    lhsT_scale=e_scales[b][:, j * P : (j + 1) * P],
                    rhs=v_codes[b][:, cols].bitcast(FP8X4),
                    rhs_scale=v_scales[b][:, cols],
                    start=True,
                    stop=True,
                )
            units = slice(b * BLOCKS, (b + 1) * BLOCKS)
            if on_vector:
                nc.vector.tensor_tensor(
                    out=o_tiles[b][:, :, cols],
                    in0=bank[:],
                    in1=row_scale[:, units].unsqueeze(2).to_broadcast([P, BLOCKS, P]),
                    op=ALU.mult,
                )
            else:
                for j in range(BLOCKS):
                    nc.scalar.activation(
                        out=o_tiles[b][:, j, cols],
                        in_=bank[:, j, :],
                        func=ACT.Copy,
                        scale=row_scale[:, b * BLOCKS + j : b * BLOCKS + j + 1],
                    )
            nc.sync.dma_start(
                out=out[b].rearrange("(p j) h -> p j h", j=BLOCKS)[:, :, cols],
                in_=o_tiles[b][:, :, cols],
            )

        def attend(b):
            o_sb = batch_pool.tile([P, BLOCKS, H], F32, name="o_sb")
            for j0 in range(0, BLOCKS, 2):
                bank = work_psum.tile([P, 2, H], F32, name="o_bank", tag="work")
                for i in range(2):
                    j = j0 + i
                    nc.tensor.matmul_mx(
                        out=bank[:, i, :],
                        lhsT=e_codes[b][:, j * P : (j + 1) * P].bitcast(FP8X4),
                        lhsT_scale=e_scales[b][:, j * P : (j + 1) * P],
                        rhs=v_codes[b][:].bitcast(FP8X4),
                        rhs_scale=v_scales[b][:],
                        start=True,
                        stop=True,
                    )
                unit = b * BLOCKS + j0
                if j0 == 0:
                    nc.vector.tensor_tensor(
                        out=o_sb[:, j0 : j0 + 2, :],
                        in0=bank[:],
                        in1=row_scale[:, unit : unit + 2].unsqueeze(2).to_broadcast([P, 2, H]),
                        op=ALU.mult,
                    )
                else:
                    for i in range(2):
                        nc.scalar.activation(
                            out=o_sb[:, j0 + i, :],
                            in_=bank[:, i, :],
                            func=ACT.Copy,
                            scale=row_scale[:, unit + i : unit + i + 1],
                        )
                nc.sync.dma_start(
                    out=out[b].rearrange("(p j) h -> p j h", j=BLOCKS)[:, j0 : j0 + 2, :],
                    in_=o_sb[:, j0 : j0 + 2, :],
                )
        warm_bank = work_psum.tile([P, P], F32, name="warm_bank", tag="work")
        for i in range(WARM_UP):
            nc.tensor.matmul(out=warm_bank[:], lhsT=ones[:], rhs=ones[:], start=True, stop=True)
        for b in range(B):
            flip_k_and_q(b)
        spread_rows()
        qk_matmuls(0)
        floors(0)
        floors(1)
        floors(2)
        floors(3)
        logs(0)
        logs(1)
        sort_words(0)
        transpose_round(0)
        add_prior(0)
        row_maxima(0)
        qk_matmuls(1)
        logs(2)
        logs(3)
        add_prior(1)
        sort_words(1)
        transpose_round(1)
        quantise_round(0)
        row_maxima(1)
        qk_matmuls(2)
        add_prior(2)
        passes_round(0)
        qk_matmuls(3)
        quantise_round(1)
        add_prior(3)
        row_maxima(2)
        exponentials(0)
        load_x(6)
        sort_words(2)
        transpose_round(2)
        passes_round(1)
        row_maxima(3)
        load_x(7)
        sort_words(3)
        transpose_round(3)
        sort_words(4)
        exponentials(1)
        quantise_round(2)
        for r in range(4, ROUNDS):
            if r + 4 < ROUNDS:
                load_x(r + 4)
            if r + 1 < ROUNDS:
                sort_words(r + 1)
            quantise_round(r - 1)
            if r in (6, 10, 14):
                finish_blocks((r - 6) // 8, (r - 6) // 2 % 4, 2)
            if r == 11:
                group_v(0)
            if r == 12:
                quantise_v(0)
            if r == 13:
                quantise_e(1)
            for half in range(2):
                transpose_round(r, range(half * ROUND_BANKS // 2, (half + 1) * ROUND_BANKS // 2))
                passes_round(
                    r - PASS_LAG,
                    groups=range(half * ROUND_GROUPS // 2, (half + 1) * ROUND_GROUPS // 2),
                )
            if r in (5, 7, 9, 11):
                exponential((r + 3) // 2)
            if r in (8, 10, 12, 14):
                transpose_e((r - 8) // 2)
        quantise_round(ROUNDS - 1, 0, ROUND_GROUPS // 2)
        finish_blocks(1, 2, 1)
        quantise_round(ROUNDS - 1, ROUND_GROUPS // 2, ROUND_GROUPS)
        quantise_e(3)
        attend(0)
        low, high = slice(0, P), slice(P, H)
        passes_round(ROUNDS - 2, low)
        passes_round(ROUNDS - 1, low)
        high_bank = work_psum.tile([P, P], F32, name="high_bank", tag="work")
        passes_round(ROUNDS - 2, high, high_bank)
        passes_round(ROUNDS - 1, high, high_bank)
        finish_blocks(1, 3, 1, low)
        group_v(1, low)
        quantise_v(1, low)
        attend_half(1, low, False)
        finish_blocks(1, 3, 1, high, high_bank)
        group_v(1, high)
        quantise_v(1, high)
        attend_half(1, high, True)
